import numpy as np
import ml_dtypes


def mxq(x, axis, fmt="e4m3"):
    dtype, down = {"e4m3": (ml_dtypes.float8_e4m3fn, 7), "e5m2": (ml_dtypes.float8_e5m2, 14)}[fmt]
    v = np.moveaxis(np.asarray(x, np.float32).astype(ml_dtypes.bfloat16).astype(np.float64), axis, -1)
    blocks = v.reshape(v.shape[:-1] + (-1, 32))
    amax = np.abs(blocks).max(-1, keepdims=True)
    byte = np.maximum(np.where(amax > 0, np.frexp(amax)[1] - 1 + 127, 0) - down, 1)
    scale = np.exp2(byte - 127.0)
    codes = (blocks / scale).astype(np.float32).astype(dtype).astype(np.float64)
    return np.moveaxis((codes * scale).reshape(v.shape), -1, axis)


WIDE = False


def mx_kscale(k):
    if not WIDE:
        return np.ones(k)
    levels = np.array([10, -10, 5, -5, 0])
    a = np.random.permutation(np.resize(levels, k // 512 * 4)).reshape(k // 512, 4)
    idx = np.arange(k)
    return np.exp2(a[idx // 512, idx % 128 // 32])


BF16 = ml_dtypes.bfloat16


def bf(x):
    return np.asarray(x, np.float32).astype(BF16)


def f64(x):
    return np.asarray(x).astype(np.float64)


C, H, W = 512, 64, 64
N = H * W


def softmax_rows(s):
    e = np.exp(s - s.max(-1, keepdims=True))
    return e / e.sum(-1, keepdims=True)


def setup_inputs():
    s = mx_kscale(C)
    return {"score_f": bf(np.random.standard_normal((C, C)) * 2.0),
            "score_l": bf(np.random.standard_normal((C, C)) * 2.0),
            "x_m": bf(np.random.standard_normal((C, N)) * s[:, None]),
            "Wv": bf(np.random.standard_normal((C, C)) * 2.0 / np.sqrt(C) / s),
            "bv": bf(np.random.standard_normal(C) * 0.5),
            "gamma": bf(2.0 + 0.2 * np.random.standard_normal(1)),
            "x_f": bf(np.random.standard_normal((C, N))),
            "x_l": bf(np.random.standard_normal((C, N)))}


def reference(score_f, score_l, x_m, Wv, bv, gamma, x_f, x_l):
    att_f = mxq(softmax_rows(f64(score_f)), 1, "e4m3")
    att_l = mxq(softmax_rows(f64(score_l)), 1, "e4m3")
    v = mxq((mxq(f64(Wv), 1, "e4m3") @ mxq(f64(x_m), 0, "e4m3")) + f64(bv)[:, None], 0, "e4m3")
    o = (att_f @ v) + (att_l @ v)
    return f64(gamma) * o + (f64(x_l) + f64(x_f)) / 2

@@ -1,0 +1,237 @@
+from contextlib import ExitStack
+
+import concourse.mybir as mybir
+from concourse.masks import make_identity
+
+BF16 = mybir.dt.bfloat16
+F32 = mybir.dt.float32
+U32 = mybir.dt.uint32
+U8 = mybir.dt.uint8
+FP8X4 = mybir.dt.float8_e4m3fn_x4
+ALU = mybir.AluOpType
+ACT = mybir.ActivationFunctionType
+AXIS = mybir.AxisListType
+
+P = 128
+PACK = 4
+C = P * PACK
+PIXELS = 4096
+CHUNK = 512
+N_CHUNKS = PIXELS // CHUNK
+SUB = CHUNK // PACK
+PIECE = 1024
+CHUNKS_PER_PIECE = PIECE // CHUNK
+N_PIECES = PIXELS // PIECE
+
+FLOPS = 3 * 2 * C * C * PIXELS
+
+
+def pack_transposed(nc, psum, sbuf, identity, rows, which, copy):
+    grouped = sbuf.tile([P, PACK, P, PACK], BF16, name="grouped_" + which, align_bytes=64)
+    for j in range(PACK):
+        flipped = psum.tile([P, PACK, P], BF16, name="flipped", tag="o")
+        for t in range(PACK):
+            nc.tensor.transpose(flipped[:, t, :], rows[:, j, t, :], identity[:])
+        copy(out=grouped[:, j, :, :], in_=flipped[:].rearrange("q t p -> q p t"))
+    codes = sbuf.tile([P, C], U32, name="codes_" + which, align_bytes=64)
+    scales = sbuf.tile([P, C], U8, name="scales_" + which, align_bytes=64)
+    nc.vector.quantize_mx(
+        out=codes[:].bitcast(FP8X4),
+        scales=scales[:],
+        in_=grouped[:].rearrange("q j p t -> q (j p t)"),
+    )
+    return codes, scales
+
+
+def softmax_rows(nc, sbuf, score, which):
+    negmax = sbuf.tile([P, PACK], F32, name="negmax_" + which)
+    nc.vector.tensor_reduce(out=negmax[:], in_=score[:], axis=AXIS.X, op=ALU.max, negate=True)
+    e = sbuf.tile([P, PACK, PACK, P], F32, name="e_" + which)
+    rowsum = sbuf.tile([P, PACK], F32, name="rowsum_" + which)
+    for j in range(PACK):
+        nc.scalar.activation(
+            out=e[:, j, :, :].rearrange("p t q -> p q t"),
+            in_=score[:, j, :].rearrange("p (q t) -> p q t", t=PACK),
+            func=ACT.Exp,
+            bias=negmax[:, j : j + 1],
+            scale=1.0,
+            accum_out=rowsum[:, j : j + 1],
+        )
+    inverse = sbuf.tile([P, PACK], F32, name="inverse_" + which)
+    nc.vector.reciprocal(out=inverse[:], in_=rowsum[:])
+    att = sbuf.tile([P, PACK, PACK, P], BF16, name="att_" + which)
+    for j in range(PACK):
+        nc.vector.tensor_scalar_mul(
+            out=att[:, j, :, :], in0=e[:, j, :, :], scalar1=inverse[:, j : j + 1]
+        )
+    return att
+
+
+def tile_coatten2_pb_t_kernel(tc, score_f, score_l, x_m, Wv, bv, gamma, x_f, x_l, out):
+    nc = tc.nc
+    with ExitStack() as stack:
+        keep = stack.enter_context(tc.tile_pool(name="keep", bufs=1))
+        work = stack.enter_context(tc.tile_pool(name="work", bufs=2))
+        frames = stack.enter_context(tc.tile_pool(name="frames", bufs=4))
+        psum = stack.enter_context(tc.psum_pool(name="psum", bufs=4))
+
+        identity = keep.tile([P, P], BF16, name="identity")
+        make_identity(nc, identity[:])
+
+        def by_rows(matrix):
+            return matrix.rearrange("(p j) n -> p j n", j=PACK)
+
+        bias_bf = keep.tile([P, PACK], BF16, name="bias_bf")
+        nc.scalar.dma_start(out=bias_bf[:], in_=bv.rearrange("(p t) -> p t", t=PACK))
+        gamma_bf = keep.tile([P, 1], BF16, name="gamma_bf")
+        nc.scalar.dma_start(out=gamma_bf[:], in_=gamma.partition_broadcast(P))
+
+        def load_piece(matrix, which, k):
+            piece = keep.tile([P, PACK, PIECE], BF16, name="%s_%d" % (which, k))
+            nc.sync.dma_start(out=piece[:], in_=by_rows(matrix)[:, :, k * PIECE : (k + 1) * PIECE])
+            return piece
+
+        wv_rows = keep.tile([P, PACK, C], BF16, name="wv_rows")
+        nc.sync.dma_start(out=wv_rows[:], in_=by_rows(Wv))
+        xm_pieces = [load_piece(x_m, "xm", 0)]
+        score_f_rows = keep.tile([P, PACK, C], BF16, name="score_f_rows")
+        nc.sync.dma_start(out=score_f_rows[:], in_=by_rows(score_f))
+        score_l_rows = keep.tile([P, PACK, C], BF16, name="score_l_rows")
+        nc.sync.dma_start(out=score_l_rows[:], in_=by_rows(score_l))
+        xl_pieces = []
+        xf_pieces = []
+        for k in range(N_PIECES):
+            if k > 0:
+                xm_pieces.append(load_piece(x_m, "xm", k))
+            xl_pieces.append(load_piece(x_l, "xl", k))
+            xf_pieces.append(load_piece(x_f, "xf", k))
+
+        def chunk_of(pieces, i):
+            first = (i % CHUNKS_PER_PIECE) * CHUNK
+            return pieces[i // CHUNKS_PER_PIECE][:, :, first : first + CHUNK]
+
+        bias = keep.tile([P, PACK], F32, name="bias")
+        nc.vector.tensor_copy(out=bias[:], in_=bias_bf[:])
+        gain = keep.tile([P, 1], F32, name="gain")
+        nc.vector.tensor_copy(out=gain[:], in_=gamma_bf[:])
+
+        wv_sorted = keep.tile([P, PACK, PACK, P], BF16, name="wv_sorted")
+        nc.vector.tensor_copy(
+            out=wv_sorted[:], in_=wv_rows[:].rearrange("p j (q t) -> p j t q", t=PACK)
+        )
+        wv_codes, wv_scales = pack_transposed(
+            nc, psum, keep, identity, wv_sorted, "wv", nc.vector.tensor_copy
+        )
+        att_f = softmax_rows(nc, keep, score_f_rows, "f")
+        att_l = softmax_rows(nc, keep, score_l_rows, "l")
+        f_codes, f_scales = pack_transposed(nc, psum, keep, identity, att_f, "f", nc.scalar.copy)
+        l_codes, l_scales = pack_transposed(nc, psum, keep, identity, att_l, "l", nc.scalar.copy)
+
+        x_grouped = {}
+        x_packed = {}
+        v_grouped = {}
+        v_packed = {}
+        frame = {}
+
+        def quantise(grouped, which):
+            codes = work.tile([P, CHUNK], U32, name=which + "_codes", align_bytes=64)
+            scales = work.tile([P, CHUNK], U8, name=which + "_scales", align_bytes=64)
+            nc.vector.quantize_mx(
+                out=codes[:].bitcast(FP8X4),
+                scales=scales[:],
+                in_=grouped[:].rearrange("p n t -> p (n t)"),
+            )
+            return codes, scales
+
+        def regroup_x(i):
+            grouped = work.tile([P, CHUNK, PACK], BF16, name="x_grouped", bufs=3, align_bytes=64)
+            nc.scalar.copy(
+                out=grouped[:].rearrange("p (c i) t -> p c t i", i=4),
+                in_=chunk_of(xm_pieces, i).rearrange("p t (c i) -> p c t i", i=4),
+            )
+            x_grouped[i] = grouped
+
+        def project(i):
+            codes, scales = x_packed[i]
+            grouped = work.tile([P, CHUNK, PACK], BF16, name="v_grouped", align_bytes=64)
+            for s in range(CHUNK // SUB):
+                pixels = slice(s * SUB, (s + 1) * SUB)
+                product = psum.tile([P, PACK, SUB], F32, name="product", tag="v")
+                for t in range(PACK):
+                    channels = slice(t * P, (t + 1) * P)
+                    nc.tensor.matmul_mx(
+                        out=product[:, t, :],
+                        lhsT=wv_codes[:, channels].bitcast(FP8X4),
+                        lhsT_scale=wv_scales[:, channels],
+                        rhs=codes[:, pixels].bitcast(FP8X4),
+                        rhs_scale=scales[:, pixels],
+                        start=True,
+                        stop=True,
+                    )
+                nc.vector.tensor_tensor(
+                    out=grouped[:, pixels, :],
+                    in0=product[:].rearrange("p t n -> p n t"),
+                    in1=bias[:].unsqueeze(1).to_broadcast([P, SUB, PACK]),
+                    op=ALU.add,
+                )
+            v_grouped[i] = grouped
+
+        def mean_frames(i):
+            mean = frames.tile([P, PACK, CHUNK], F32, name="frame")
+            nc.gpsimd.tensor_tensor(
+                out=mean[:], in0=chunk_of(xl_pieces, i), in1=chunk_of(xf_pieces, i), op=ALU.add
+            )
+            nc.scalar.mul(out=mean[:], in_=mean[:], mul=0.5)
+            frame[i] = mean
+
+        def attend(i):
+            codes, scales = v_packed[i]
+            for j in range(PACK):
+                channels = slice(j * P, (j + 1) * P)
+                attended = psum.tile([P, CHUNK], F32, name="attended", tag="o")
+                nc.tensor.matmul_mx(
+                    out=attended[:],
+                    lhsT=f_codes[:, channels].bitcast(FP8X4),
+                    lhsT_scale=f_scales[:, channels],
+                    rhs=codes[:].bitcast(FP8X4),
+                    rhs_scale=scales[:],
+                    start=True,
+                    stop=False,
+                )
+                nc.tensor.matmul_mx(
+                    out=attended[:],
+                    lhsT=l_codes[:, channels].bitcast(FP8X4),
+                    lhsT_scale=l_scales[:, channels],
+                    rhs=codes[:].bitcast(FP8X4),
+                    rhs_scale=scales[:],
+                    start=False,
+                    stop=True,
+                )
+                nc.vector.scalar_tensor_tensor(
+                    out=frame[i][:, j, :],
+                    in0=attended[:],
+                    scalar=gain[:, 0:1],
+                    in1=frame[i][:, j, :],
+                    op0=ALU.mult,
+                    op1=ALU.add,
+                )
+            nc.sync.dma_start(
+                out=by_rows(out)[:, :, i * CHUNK : (i + 1) * CHUNK], in_=frame[i][:]
+            )
+
+        def chunks(i):
+            return 0 <= i < N_CHUNKS
+
+        for step in range(N_CHUNKS + 3):
+            if chunks(step):
+                regroup_x(step)
+            if chunks(step - 1):
+                mean_frames(step - 1)
+            if chunks(step - 2):
+                project(step - 2)
+            if chunks(step - 1):
+                x_packed[step - 1] = quantise(x_grouped[step - 1], "x")
+            if chunks(step - 2):
+                v_packed[step - 2] = quantise(v_grouped[step - 2], "v")
+            if chunks(step - 3):
+                attend(step - 3)

@@ -178,9 +178,13 @@ def tile_coatten2_pb_t_kernel(tc, score_f, score_l, x_m, Wv, bv, gamma, x_f, x_l
 
         def mean_frames(i):
             mean = frames.tile([P, PACK, CHUNK], F32, name="frame")
-            nc.gpsimd.tensor_tensor(
-                out=mean[:], in0=chunk_of(xl_pieces, i), in1=chunk_of(xf_pieces, i), op=ALU.add
-            )
+            for j in range(PACK):
+                nc.gpsimd.tensor_tensor(
+                    out=mean[:, j, :],
+                    in0=chunk_of(xl_pieces, i)[:, j, :],
+                    in1=chunk_of(xf_pieces, i)[:, j, :],
+                    op=ALU.add,
+                )
             nc.scalar.mul(out=mean[:], in_=mean[:], mul=0.5)
             frame[i] = mean
 

@@ -19,20 +19,41 @@ PIXELS = 4096
 CHUNK = 512
 N_CHUNKS = PIXELS // CHUNK
 SUB = CHUNK // PACK
+N_BANKS = N_CHUNKS * PACK
 PIECE = 1024
 CHUNKS_PER_PIECE = PIECE // CHUNK
 N_PIECES = PIXELS // PIECE
+AHEAD = 3
+LAG = 8
+VECTOR_REGROUPS = 2
+TENSOR_MEANS = 2
 
 FLOPS = 3 * 2 * C * C * PIXELS
 
 
-def pack_transposed(nc, psum, sbuf, identity, rows, which, copy):
+def flip(nc, psum, sbuf, identity, rows, which, copy):
     grouped = sbuf.tile([P, PACK, P, PACK], BF16, name="grouped_" + which, align_bytes=64)
     for j in range(PACK):
         flipped = psum.tile([P, PACK, P], BF16, name="flipped", tag="o")
         for t in range(PACK):
             nc.tensor.transpose(flipped[:, t, :], rows[:, j, t, :], identity[:])
         copy(out=grouped[:, j, :, :], in_=flipped[:].rearrange("q t p -> q p t"))
+    return grouped
+
+
+def flip_words(nc, psum, sbuf, identity_f32, rows, which, copy):
+    words = rows[:].bitcast(F32).rearrange("p j (q u) -> p j u q", u=2)
+    grouped = sbuf.tile([P, PACK, P, PACK], BF16, name="grouped_" + which, align_bytes=64)
+    grouped_words = grouped[:].bitcast(F32)
+    for j in range(PACK):
+        flipped = psum.tile([P, 2, P], F32, name="flipped_words", tag="o")
+        for u in range(2):
+            nc.tensor.transpose(flipped[:, u, :], words[:, j, u, :], identity_f32[:])
+        copy(out=grouped_words[:, j, :, :], in_=flipped[:].rearrange("q u p -> q p u"))
+    return grouped
+
+
+def quantise_matrix(nc, sbuf, grouped, which):
     codes = sbuf.tile([P, C], U32, name="codes_" + which, align_bytes=64)
     scales = sbuf.tile([P, C], U8, name="scales_" + which, align_bytes=64)
     nc.vector.quantize_mx(
@@ -43,7 +64,7 @@ def pack_transposed(nc, psum, sbuf, identity, rows, which, copy):
     return codes, scales
 
 
-def softmax_rows(nc, sbuf, score, which):
+def exponentials(nc, sbuf, score, which):
     negmax = sbuf.tile([P, PACK], F32, name="negmax_" + which)
     nc.vector.tensor_reduce(out=negmax[:], in_=score[:], axis=AXIS.X, op=ALU.max, negate=True)
     e = sbuf.tile([P, PACK, PACK, P], F32, name="e_" + which)
@@ -57,12 +78,17 @@ def softmax_rows(nc, sbuf, score, which):
             scale=1.0,
             accum_out=rowsum[:, j : j + 1],
         )
+    return e, rowsum
+
+
+def normalise(nc, sbuf, e, rowsum, which):
     inverse = sbuf.tile([P, PACK], F32, name="inverse_" + which)
     nc.vector.reciprocal(out=inverse[:], in_=rowsum[:])
     att = sbuf.tile([P, PACK, PACK, P], BF16, name="att_" + which)
     for j in range(PACK):
-        nc.vector.tensor_scalar_mul(
-            out=att[:, j, :, :], in0=e[:, j, :, :], scalar1=inverse[:, j : j + 1]
+        nc.gpsimd.tensor_scalar(
+            out=att[:, j, :, :], in0=e[:, j, :, :], scalar1=inverse[:, j : j + 1], scalar2=0.0,
+            op0=ALU.mult, op1=ALU.add,
         )
     return att
 
@@ -70,13 +96,18 @@ def softmax_rows(nc, sbuf, score, which):
 def tile_coatten2_pb_t_kernel(tc, score_f, score_l, x_m, Wv, bv, gamma, x_f, x_l, out):
     nc = tc.nc
     with ExitStack() as stack:
+        stack.enter_context(tc.manual_schedule())
         keep = stack.enter_context(tc.tile_pool(name="keep", bufs=1))
         work = stack.enter_context(tc.tile_pool(name="work", bufs=2))
         frames = stack.enter_context(tc.tile_pool(name="frames", bufs=4))
-        psum = stack.enter_context(tc.psum_pool(name="psum", bufs=4))
+        psum = stack.enter_context(tc.psum_pool(name="psum", bufs=AHEAD))
 
         identity = keep.tile([P, P], BF16, name="identity")
         make_identity(nc, identity[:])
+        identity_f32 = keep.tile([P, P], F32, name="identity_f32")
+        make_identity(nc, identity_f32[:])
+        half_identity = keep.tile([P, P], BF16, name="half_identity")
+        nc.vector.tensor_scalar_mul(out=half_identity[:], in0=identity[:], scalar1=0.5)
 
         def by_rows(matrix):
             return matrix.rearrange("(p j) n -> p j n", j=PACK)
@@ -86,18 +117,20 @@ def tile_coatten2_pb_t_kernel(tc, score_f, score_l, x_m, Wv, bv, gamma, x_f, x_l
         gamma_bf = keep.tile([P, 1], BF16, name="gamma_bf")
         nc.scalar.dma_start(out=gamma_bf[:], in_=gamma.partition_broadcast(P))
 
+        def load_matrix(matrix, which):
+            rows = keep.tile([P, PACK, C], BF16, name=which + "_rows")
+            nc.sync.dma_start(out=rows[:], in_=by_rows(matrix))
+            return rows
+
         def load_piece(matrix, which, k):
             piece = keep.tile([P, PACK, PIECE], BF16, name="%s_%d" % (which, k))
             nc.sync.dma_start(out=piece[:], in_=by_rows(matrix)[:, :, k * PIECE : (k + 1) * PIECE])
             return piece
 
-        wv_rows = keep.tile([P, PACK, C], BF16, name="wv_rows")
-        nc.sync.dma_start(out=wv_rows[:], in_=by_rows(Wv))
+        score_f_rows = load_matrix(score_f, "score_f")
+        score_l_rows = load_matrix(score_l, "score_l")
+        wv_rows = load_matrix(Wv, "wv")
         xm_pieces = [load_piece(x_m, "xm", 0)]
-        score_f_rows = keep.tile([P, PACK, C], BF16, name="score_f_rows")
-        nc.sync.dma_start(out=score_f_rows[:], in_=by_rows(score_f))
-        score_l_rows = keep.tile([P, PACK, C], BF16, name="score_l_rows")
-        nc.sync.dma_start(out=score_l_rows[:], in_=by_rows(score_l))
         xl_pieces = []
         xf_pieces = []
         for k in range(N_PIECES):
@@ -115,23 +148,14 @@ def tile_coatten2_pb_t_kernel(tc, score_f, score_l, x_m, Wv, bv, gamma, x_f, x_l
         gain = keep.tile([P, 1], F32, name="gain")
         nc.vector.tensor_copy(out=gain[:], in_=gamma_bf[:])
 
-        wv_sorted = keep.tile([P, PACK, PACK, P], BF16, name="wv_sorted")
-        nc.vector.tensor_copy(
-            out=wv_sorted[:], in_=wv_rows[:].rearrange("p j (q t) -> p j t q", t=PACK)
-        )
-        wv_codes, wv_scales = pack_transposed(
-            nc, psum, keep, identity, wv_sorted, "wv", nc.vector.tensor_copy
-        )
-        att_f = softmax_rows(nc, keep, score_f_rows, "f")
-        att_l = softmax_rows(nc, keep, score_l_rows, "l")
-        f_codes, f_scales = pack_transposed(nc, psum, keep, identity, att_f, "f", nc.scalar.copy)
-        l_codes, l_scales = pack_transposed(nc, psum, keep, identity, att_l, "l", nc.scalar.copy)
-
         x_grouped = {}
         x_packed = {}
         v_grouped = {}
         v_packed = {}
         frame = {}
+        product = {}
+        attended = {}
+        stationary = {}
 
         def quantise(grouped, which):
             codes = work.tile([P, CHUNK], U32, name=which + "_codes", align_bytes=64)
@@ -144,98 +168,136 @@ def tile_coatten2_pb_t_kernel(tc, score_f, score_l, x_m, Wv, bv, gamma, x_f, x_l
             return codes, scales
 
         def regroup_x(i):
-            grouped = work.tile([P, CHUNK, PACK], BF16, name="x_grouped", bufs=3, align_bytes=64)
-            nc.scalar.copy(
-                out=grouped[:].rearrange("p (c i) t -> p c t i", i=4),
+            x_grouped[i] = work.tile([P, CHUNK, PACK], BF16, name="x_grouped", align_bytes=64)
+            copy = nc.vector.tensor_copy if i < VECTOR_REGROUPS else nc.scalar.copy
+            copy(
+                out=x_grouped[i][:].rearrange("p (c i) t -> p c t i", i=4),
                 in_=chunk_of(xm_pieces, i).rearrange("p t (c i) -> p c t i", i=4),
             )
-            x_grouped[i] = grouped
 
-        def project(i):
+        def project(u):
+            i, s = divmod(u, PACK)
             codes, scales = x_packed[i]
-            grouped = work.tile([P, CHUNK, PACK], BF16, name="v_grouped", align_bytes=64)
-            for s in range(CHUNK // SUB):
-                pixels = slice(s * SUB, (s + 1) * SUB)
-                product = psum.tile([P, PACK, SUB], F32, name="product", tag="v")
-                for t in range(PACK):
-                    channels = slice(t * P, (t + 1) * P)
-                    nc.tensor.matmul_mx(
-                        out=product[:, t, :],
-                        lhsT=wv_codes[:, channels].bitcast(FP8X4),
-                        lhsT_scale=wv_scales[:, channels],
-                        rhs=codes[:, pixels].bitcast(FP8X4),
-                        rhs_scale=scales[:, pixels],
-                        start=True,
-                        stop=True,
-                    )
-                nc.vector.tensor_tensor(
-                    out=grouped[:, pixels, :],
-                    in0=product[:].rearrange("p t n -> p n t"),
-                    in1=bias[:].unsqueeze(1).to_broadcast([P, SUB, PACK]),
-                    op=ALU.add,
+            wv_codes, wv_scales = stationary["wv"]
+            pixels = slice(s * SUB, (s + 1) * SUB)
+            product[u] = psum.tile([P, PACK, SUB], F32, name="product", tag="v")
+            for t in range(PACK):
+                channels = slice(t * P, (t + 1) * P)
+                nc.tensor.matmul_mx(
+                    out=product[u][:, t, :],
+                    lhsT=wv_codes[:, channels].bitcast(FP8X4),
+                    lhsT_scale=wv_scales[:, channels],
+                    rhs=codes[:, pixels].bitcast(FP8X4),
+                    rhs_scale=scales[:, pixels],
+                    start=True,
+                    stop=True,
                 )
-            v_grouped[i] = grouped
+
+        def add_bias(u):
+            i, s = divmod(u, PACK)
+            if s == 0:
+                v_grouped[i] = work.tile([P, CHUNK, PACK], BF16, name="v_grouped", align_bytes=64)
+            nc.vector.tensor_tensor(
+                out=v_grouped[i][:, s * SUB : (s + 1) * SUB, :],
+                in0=product[u][:].rearrange("p t n -> p n t"),
+                in1=bias[:].unsqueeze(1).to_broadcast([P, SUB, PACK]),
+                op=ALU.add,
+            )
 
         def mean_frames(i):
-            mean = frames.tile([P, PACK, CHUNK], F32, name="frame")
-            for j in range(PACK):
+            frame[i] = frames.tile([P, PACK, CHUNK], F32, name="frame")
+            for j in range(TENSOR_MEANS):
+                mean = psum.tile([P, CHUNK], F32, name="mean", tag="m", bufs=2)
+                nc.tensor.matmul(
+                    out=mean[:], lhsT=half_identity[:], rhs=chunk_of(xl_pieces, i)[:, j, :],
+                    start=True, stop=False,
+                )
+                nc.tensor.matmul(
+                    out=mean[:], lhsT=half_identity[:], rhs=chunk_of(xf_pieces, i)[:, j, :],
+                    start=False, stop=True,
+                )
+                nc.scalar.copy(out=frame[i][:, j, :], in_=mean[:])
+            for j in range(TENSOR_MEANS, PACK):
                 nc.gpsimd.tensor_tensor(
-                    out=mean[:, j, :],
+                    out=frame[i][:, j, :],
                     in0=chunk_of(xl_pieces, i)[:, j, :],
                     in1=chunk_of(xf_pieces, i)[:, j, :],
                     op=ALU.add,
                 )
-            nc.scalar.mul(out=mean[:], in_=mean[:], mul=0.5)
-            frame[i] = mean
-
-        def attend(i):
-            codes, scales = v_packed[i]
-            for j in range(PACK):
-                channels = slice(j * P, (j + 1) * P)
-                attended = psum.tile([P, CHUNK], F32, name="attended", tag="o")
-                nc.tensor.matmul_mx(
-                    out=attended[:],
-                    lhsT=f_codes[:, channels].bitcast(FP8X4),
-                    lhsT_scale=f_scales[:, channels],
-                    rhs=codes[:].bitcast(FP8X4),
-                    rhs_scale=scales[:],
-                    start=True,
-                    stop=False,
-                )
-                nc.tensor.matmul_mx(
-                    out=attended[:],
-                    lhsT=l_codes[:, channels].bitcast(FP8X4),
-                    lhsT_scale=l_scales[:, channels],
-                    rhs=codes[:].bitcast(FP8X4),
-                    rhs_scale=scales[:],
-                    start=False,
-                    stop=True,
-                )
-                nc.vector.scalar_tensor_tensor(
-                    out=frame[i][:, j, :],
-                    in0=attended[:],
-                    scalar=gain[:, 0:1],
-                    in1=frame[i][:, j, :],
-                    op0=ALU.mult,
-                    op1=ALU.add,
-                )
-            nc.sync.dma_start(
-                out=by_rows(out)[:, :, i * CHUNK : (i + 1) * CHUNK], in_=frame[i][:]
+            nc.scalar.mul(
+                out=frame[i][:, TENSOR_MEANS:, :], in_=frame[i][:, TENSOR_MEANS:, :], mul=0.5
             )
 
-        def chunks(i):
+        def attend(u):
+            i, j = divmod(u, PACK)
+            codes, scales = v_packed[i]
+            channels = slice(j * P, (j + 1) * P)
+            attended[u] = psum.tile([P, CHUNK], F32, name="attended", tag="o")
+            for which in ("f", "l"):
+                att_codes, att_scales = stationary[which]
+                nc.tensor.matmul_mx(
+                    out=attended[u][:],
+                    lhsT=att_codes[:, channels].bitcast(FP8X4),
+                    lhsT_scale=att_scales[:, channels],
+                    rhs=codes[:].bitcast(FP8X4),
+                    rhs_scale=scales[:],
+                    start=(which == "f"),
+                    stop=(which == "l"),
+                )
+
+        def fuse(u):
+            i, j = divmod(u, PACK)
+            nc.vector.scalar_tensor_tensor(
+                out=frame[i][:, j, :],
+                in0=attended[u][:],
+                scalar=gain[:, 0:1],
+                in1=frame[i][:, j, :],
+                op0=ALU.mult,
+                op1=ALU.add,
+            )
+
+        def store(i):
+            nc.sync.dma_start(out=by_rows(out)[:, :, i * CHUNK : (i + 1) * CHUNK], in_=frame[i][:])
+
+        def is_chunk(i):
             return 0 <= i < N_CHUNKS
 
-        for step in range(N_CHUNKS + 3):
-            if chunks(step):
-                regroup_x(step)
-            if chunks(step - 1):
-                mean_frames(step - 1)
-            if chunks(step - 2):
-                project(step - 2)
-            if chunks(step - 1):
-                x_packed[step - 1] = quantise(x_grouped[step - 1], "x")
-            if chunks(step - 2):
-                v_packed[step - 2] = quantise(v_grouped[step - 2], "v")
-            if chunks(step - 3):
-                attend(step - 3)
+        def is_bank(u):
+            return 0 <= u < N_BANKS
+
+        def cycle(n):
+            if is_chunk(n + 2):
+                regroup_x(n + 2)
+            if is_chunk(n - 1):
+                mean_frames(n - 1)
+            for u in range(n * PACK, (n + 1) * PACK):
+                if is_bank(u):
+                    add_bias(u)
+                if is_bank(u + AHEAD):
+                    project(u + AHEAD)
+                if is_bank(u - LAG):
+                    fuse(u - LAG)
+                if is_bank(u - LAG + AHEAD):
+                    attend(u - LAG + AHEAD)
+            if is_chunk(n - LAG // PACK):
+                store(n - LAG // PACK)
+            if is_chunk(n):
+                v_packed[n] = quantise(v_grouped[n], "v")
+            if is_chunk(n + 2):
+                x_packed[n + 2] = quantise(x_grouped[n + 2], "x")
+
+        e_f, sum_f = exponentials(nc, keep, score_f_rows, "f")
+        e_l, sum_l = exponentials(nc, keep, score_l_rows, "l")
+        wv_grouped = flip_words(nc, psum, keep, identity_f32, wv_rows, "wv", nc.vector.tensor_copy)
+        stationary["wv"] = quantise_matrix(nc, keep, wv_grouped, "wv")
+        att_f = normalise(nc, keep, e_f, sum_f, "f")
+        cycle(-2)
+        att_l = normalise(nc, keep, e_l, sum_l, "l")
+        cycle(-1)
+        f_grouped = flip(nc, psum, keep, identity, att_f, "f", nc.scalar.copy)
+        cycle(0)
+        l_grouped = flip(nc, psum, keep, identity, att_l, "l", nc.scalar.copy)
+        stationary["f"] = quantise_matrix(nc, keep, f_grouped, "f")
+        stationary["l"] = quantise_matrix(nc, keep, l_grouped, "l")
+        for n in range(1, N_CHUNKS + LAG // PACK):
+            cycle(n)

@@ -130,14 +130,14 @@ def tile_coatten2_pb_t_kernel(tc, score_f, score_l, x_m, Wv, bv, gamma, x_f, x_l
         score_f_rows = load_matrix(score_f, "score_f")
         score_l_rows = load_matrix(score_l, "score_l")
         wv_rows = load_matrix(Wv, "wv")
-        xm_pieces = [load_piece(x_m, "xm", 0)]
+        xm_pieces = [load_piece(x_m, "xm", 0), load_piece(x_m, "xm", 1)]
         xl_pieces = []
         xf_pieces = []
         for k in range(N_PIECES):
-            if k > 0:
-                xm_pieces.append(load_piece(x_m, "xm", k))
             xl_pieces.append(load_piece(x_l, "xl", k))
             xf_pieces.append(load_piece(x_f, "xf", k))
+            if k + 2 < N_PIECES:
+                xm_pieces.append(load_piece(x_m, "xm", k + 2))
 
         def chunk_of(pieces, i):
             first = (i % CHUNKS_PER_PIECE) * CHUNK
@@ -255,9 +255,9 @@ def tile_coatten2_pb_t_kernel(tc, score_f, score_l, x_m, Wv, bv, gamma, x_f, x_l
                 op0=ALU.mult,
                 op1=ALU.add,
             )
-
-        def store(i):
-            nc.sync.dma_start(out=by_rows(out)[:, :, i * CHUNK : (i + 1) * CHUNK], in_=frame[i][:])
+            nc.sync.dma_start(
+                out=by_rows(out)[:, j, i * CHUNK : (i + 1) * CHUNK], in_=frame[i][:, j, :]
+            )
 
         def is_chunk(i):
             return 0 <= i < N_CHUNKS
@@ -279,8 +279,6 @@ def tile_coatten2_pb_t_kernel(tc, score_f, score_l, x_m, Wv, bv, gamma, x_f, x_l
                     fuse(u - LAG)
                 if is_bank(u - LAG + AHEAD):
                     attend(u - LAG + AHEAD)
-            if is_chunk(n - LAG // PACK):
-                store(n - LAG // PACK)
             if is_chunk(n):
                 v_packed[n] = quantise(v_grouped[n], "v")
             if is_chunk(n + 2):

@@ -96,7 +96,6 @@ def normalise(nc, sbuf, e, rowsum, which):
 def tile_coatten2_pb_t_kernel(tc, score_f, score_l, x_m, Wv, bv, gamma, x_f, x_l, out):
     nc = tc.nc
     with ExitStack() as stack:
-        stack.enter_context(tc.manual_schedule())
         keep = stack.enter_context(tc.tile_pool(name="keep", bufs=1))
         work = stack.enter_context(tc.tile_pool(name="work", bufs=2))
         frames = stack.enter_context(tc.tile_pool(name="frames", bufs=4))

@@ -66,10 +66,12 @@ def quantise_matrix(nc, sbuf, grouped, which):
 
 def exponentials(nc, sbuf, score, which):
     negmax = sbuf.tile([P, PACK], F32, name="negmax_" + which)
-    nc.vector.tensor_reduce(out=negmax[:], in_=score[:], axis=AXIS.X, op=ALU.max, negate=True)
     e = sbuf.tile([P, PACK, PACK, P], F32, name="e_" + which)
     rowsum = sbuf.tile([P, PACK], F32, name="rowsum_" + which)
     for j in range(PACK):
+        nc.vector.tensor_reduce(
+            out=negmax[:, j : j + 1], in_=score[:, j, :], axis=AXIS.X, op=ALU.max, negate=True
+        )
         nc.scalar.activation(
             out=e[:, j, :, :].rearrange("p t q -> p q t"),
             in_=score[:, j, :].rearrange("p (q t) -> p q t", t=PACK),
@@ -96,6 +98,7 @@ def normalise(nc, sbuf, e, rowsum, which):
 def tile_coatten2_pb_t_kernel(tc, score_f, score_l, x_m, Wv, bv, gamma, x_f, x_l, out):
     nc = tc.nc
     with ExitStack() as stack:
+        stack.enter_context(tc.manual_schedule())
         keep = stack.enter_context(tc.tile_pool(name="keep", bufs=1))
         work = stack.enter_context(tc.tile_pool(name="work", bufs=2))
         frames = stack.enter_context(tc.tile_pool(name="frames", bufs=4))
@@ -118,7 +121,8 @@ def tile_coatten2_pb_t_kernel(tc, score_f, score_l, x_m, Wv, bv, gamma, x_f, x_l
 
         def load_matrix(matrix, which):
             rows = keep.tile([P, PACK, C], BF16, name=which + "_rows")
-            nc.sync.dma_start(out=rows[:], in_=by_rows(matrix))
+            for j in range(PACK):
+                nc.sync.dma_start(out=rows[:, j, :], in_=by_rows(matrix)[:, j, :])
             return rows
 
         def load_piece(matrix, which, k):
@@ -285,11 +289,11 @@ def tile_coatten2_pb_t_kernel(tc, score_f, score_l, x_m, Wv, bv, gamma, x_f, x_l
 
         e_f, sum_f = exponentials(nc, keep, score_f_rows, "f")
         e_l, sum_l = exponentials(nc, keep, score_l_rows, "l")
+        att_f = normalise(nc, keep, e_f, sum_f, "f")
         wv_grouped = flip_words(nc, psum, keep, identity_f32, wv_rows, "wv", nc.vector.tensor_copy)
         stationary["wv"] = quantise_matrix(nc, keep, wv_grouped, "wv")
-        att_f = normalise(nc, keep, e_f, sum_f, "f")
-        cycle(-2)
         att_l = normalise(nc, keep, e_l, sum_l, "l")
+        cycle(-2)
         cycle(-1)
         f_grouped = flip(nc, psum, keep, identity, att_f, "f", nc.scalar.copy)
         cycle(0)

@@ -114,10 +114,10 @@ def tile_coatten2_pb_t_kernel(tc, score_f, score_l, x_m, Wv, bv, gamma, x_f, x_l
         def by_rows(matrix):
             return matrix.rearrange("(p j) n -> p j n", j=PACK)
 
-        bias_bf = keep.tile([P, PACK], BF16, name="bias_bf")
-        nc.scalar.dma_start(out=bias_bf[:], in_=bv.rearrange("(p t) -> p t", t=PACK))
-        gamma_bf = keep.tile([P, 1], BF16, name="gamma_bf")
-        nc.scalar.dma_start(out=gamma_bf[:], in_=gamma.partition_broadcast(P))
+        bias = keep.tile([P, PACK], BF16, name="bias")
+        nc.scalar.dma_start(out=bias[:], in_=bv.rearrange("(p t) -> p t", t=PACK))
+        gain = keep.tile([P, 1], BF16, name="gain")
+        nc.scalar.dma_start(out=gain[:], in_=gamma.partition_broadcast(P))
 
         def load_matrix(matrix, which):
             rows = keep.tile([P, PACK, C], BF16, name=which + "_rows")
@@ -145,11 +145,6 @@ def tile_coatten2_pb_t_kernel(tc, score_f, score_l, x_m, Wv, bv, gamma, x_f, x_l
         def chunk_of(pieces, i):
             first = (i % CHUNKS_PER_PIECE) * CHUNK
             return pieces[i // CHUNKS_PER_PIECE][:, :, first : first + CHUNK]
-
-        bias = keep.tile([P, PACK], F32, name="bias")
-        nc.vector.tensor_copy(out=bias[:], in_=bias_bf[:])
-        gain = keep.tile([P, 1], F32, name="gain")
-        nc.vector.tensor_copy(out=gain[:], in_=gamma_bf[:])
 
         x_grouped = {}
         x_packed = {}

@@ -20,13 +20,15 @@ CHUNK = 512
 N_CHUNKS = PIXELS // CHUNK
 SUB = CHUNK // PACK
 N_BANKS = N_CHUNKS * PACK
-PIECE = 1024
-CHUNKS_PER_PIECE = PIECE // CHUNK
-N_PIECES = PIXELS // PIECE
 AHEAD = 3
 LAG = 8
-VECTOR_REGROUPS = 2
-TENSOR_MEANS = 2
+AHEAD_O = 3
+GHALF = 5
+XLEAD = 2
+EXTRA_MEANS = 3
+RSLOTS = (0, 2)
+HSLOT = 3
+WORK_BUFS = 2
 
 FLOPS = 3 * 2 * C * C * PIXELS
 
@@ -34,7 +36,7 @@ FLOPS = 3 * 2 * C * C * PIXELS
 def flip(nc, psum, sbuf, identity, rows, which, copy):
     grouped = sbuf.tile([P, PACK, P, PACK], BF16, name="grouped_" + which, align_bytes=64)
     for j in range(PACK):
-        flipped = psum.tile([P, PACK, P], BF16, name="flipped", tag="o")
+        flipped = psum.tile([P, PACK, P], BF16, name="flipped", tag="o", bufs=AHEAD_O)
         for t in range(PACK):
             nc.tensor.transpose(flipped[:, t, :], rows[:, j, t, :], identity[:])
         copy(out=grouped[:, j, :, :], in_=flipped[:].rearrange("q t p -> q p t"))
@@ -46,7 +48,7 @@ def flip_words(nc, psum, sbuf, identity_f32, rows, which, copy):
     grouped = sbuf.tile([P, PACK, P, PACK], BF16, name="grouped_" + which, align_bytes=64)
     grouped_words = grouped[:].bitcast(F32)
     for j in range(PACK):
-        flipped = psum.tile([P, 2, P], F32, name="flipped_words", tag="o")
+        flipped = psum.tile([P, 2, P], F32, name="flipped_words", tag="o", bufs=AHEAD_O)
         for u in range(2):
             nc.tensor.transpose(flipped[:, u, :], words[:, j, u, :], identity_f32[:])
         copy(out=grouped_words[:, j, :, :], in_=flipped[:].rearrange("q u p -> q p u"))
@@ -64,14 +66,34 @@ def quantise_matrix(nc, sbuf, grouped, which):
     return codes, scales
 
 
-def exponentials(nc, sbuf, score, which):
+def row_maxima(nc, sbuf, score, which):
     negmax = sbuf.tile([P, PACK], F32, name="negmax_" + which)
+    pairs = [slice(j, j + 2) for j in range(0, PACK, 2)]
+    halves = []
+    quarters = []
+    for k, pair in enumerate(pairs):
+        half = sbuf.tile([P, 2, C // 2], BF16, name="half_%s%d" % (which, k))
+        nc.vector.tensor_tensor(
+            out=half[:], in0=score[:, pair, : C // 2], in1=score[:, pair, C // 2 :], op=ALU.max
+        )
+        halves.append(half)
+    for k, half in enumerate(halves):
+        quarter = sbuf.tile([P, 2, C // 4], BF16, name="quarter_%s%d" % (which, k))
+        nc.vector.tensor_tensor(
+            out=quarter[:], in0=half[:, :, : C // 4], in1=half[:, :, C // 4 :], op=ALU.max
+        )
+        quarters.append(quarter)
+    for pair, quarter in zip(pairs, quarters):
+        nc.vector.tensor_reduce(
+            out=negmax[:, pair], in_=quarter[:], axis=AXIS.X, op=ALU.max, negate=True
+        )
+    return negmax
+
+
+def exponentials(nc, sbuf, score, negmax, which):
     e = sbuf.tile([P, PACK, PACK, P], F32, name="e_" + which)
     rowsum = sbuf.tile([P, PACK], F32, name="rowsum_" + which)
     for j in range(PACK):
-        nc.vector.tensor_reduce(
-            out=negmax[:, j : j + 1], in_=score[:, j, :], axis=AXIS.X, op=ALU.max, negate=True
-        )
         nc.scalar.activation(
             out=e[:, j, :, :].rearrange("p t q -> p q t"),
             in_=score[:, j, :].rearrange("p (q t) -> p q t", t=PACK),
@@ -100,14 +122,14 @@ def tile_coatten2_pb_t_kernel(tc, score_f, score_l, x_m, Wv, bv, gamma, x_f, x_l
     with ExitStack() as stack:
         stack.enter_context(tc.manual_schedule())
         keep = stack.enter_context(tc.tile_pool(name="keep", bufs=1))
-        work = stack.enter_context(tc.tile_pool(name="work", bufs=2))
-        frames = stack.enter_context(tc.tile_pool(name="frames", bufs=4))
-        psum = stack.enter_context(tc.psum_pool(name="psum", bufs=AHEAD))
+        work = stack.enter_context(tc.tile_pool(name="work", bufs=WORK_BUFS))
+        frames = stack.enter_context(tc.tile_pool(name="frames", bufs=6))
+        psum = stack.enter_context(tc.psum_pool(name="psum", bufs=2))
 
-        identity = keep.tile([P, P], BF16, name="identity")
-        make_identity(nc, identity[:])
         identity_f32 = keep.tile([P, P], F32, name="identity_f32")
         make_identity(nc, identity_f32[:])
+        identity = keep.tile([P, P], BF16, name="identity")
+        make_identity(nc, identity[:])
         half_identity = keep.tile([P, P], BF16, name="half_identity")
         nc.vector.tensor_scalar_mul(out=half_identity[:], in0=identity[:], scalar1=0.5)
 
@@ -119,38 +141,41 @@ def tile_coatten2_pb_t_kernel(tc, score_f, score_l, x_m, Wv, bv, gamma, x_f, x_l
         gain = keep.tile([P, 1], BF16, name="gain")
         nc.scalar.dma_start(out=gain[:], in_=gamma.partition_broadcast(P))
 
-        def load_matrix(matrix, which):
+        def load_matrix(matrix, which, parts):
             rows = keep.tile([P, PACK, C], BF16, name=which + "_rows")
-            for j in range(PACK):
-                nc.sync.dma_start(out=rows[:, j, :], in_=by_rows(matrix)[:, j, :])
+            for j in range(0, PACK, PACK // parts):
+                part = slice(j, j + PACK // parts)
+                nc.sync.dma_start(out=rows[:, part, :], in_=by_rows(matrix)[:, part, :])
             return rows
 
-        def load_piece(matrix, which, k):
-            piece = keep.tile([P, PACK, PIECE], BF16, name="%s_%d" % (which, k))
-            nc.sync.dma_start(out=piece[:], in_=by_rows(matrix)[:, :, k * PIECE : (k + 1) * PIECE])
-            return piece
+        def load_chunk(matrix, which, k, chunks):
+            piece = keep.tile([P, PACK, chunks * CHUNK], BF16, name="%s_%d" % (which, k))
+            nc.sync.dma_start(out=piece[:], in_=by_rows(matrix)[:, :, k * CHUNK : (k + chunks) * CHUNK])
+            return [piece[:, :, c * CHUNK : (c + 1) * CHUNK] for c in range(chunks)]
 
-        score_f_rows = load_matrix(score_f, "score_f")
-        score_l_rows = load_matrix(score_l, "score_l")
-        wv_rows = load_matrix(Wv, "wv")
-        xm_pieces = [load_piece(x_m, "xm", 0), load_piece(x_m, "xm", 1)]
-        xl_pieces = []
-        xf_pieces = []
-        for k in range(N_PIECES):
-            xl_pieces.append(load_piece(x_l, "xl", k))
-            xf_pieces.append(load_piece(x_f, "xf", k))
-            if k + 2 < N_PIECES:
-                xm_pieces.append(load_piece(x_m, "xm", k + 2))
-
-        def chunk_of(pieces, i):
-            first = (i % CHUNKS_PER_PIECE) * CHUNK
-            return pieces[i // CHUNKS_PER_PIECE][:, :, first : first + CHUNK]
+        xm = load_chunk(x_m, "xm", 0, 1)
+        wv_rows = load_matrix(Wv, "wv", 4)
+        score_f_rows = load_matrix(score_f, "score_f", 2)
+        xm += load_chunk(x_m, "xm", 1, 1)
+        score_l_rows = load_matrix(score_l, "score_l", 2)
+        xm += load_chunk(x_m, "xm", 2, 1)
+        xl = load_chunk(x_l, "xl", 0, 1)
+        xf = load_chunk(x_f, "xf", 0, 1)
+        xm += load_chunk(x_m, "xm", 3, 1)
+        xl += load_chunk(x_l, "xl", 1, 1)
+        xf += load_chunk(x_f, "xf", 1, 1)
+        for k in range(2, N_CHUNKS, 2):
+            if k + 2 < N_CHUNKS:
+                xm += load_chunk(x_m, "xm", k + 2, 2)
+            xl += load_chunk(x_l, "xl", k, 2)
+            xf += load_chunk(x_f, "xf", k, 2)
 
         x_grouped = {}
         x_packed = {}
         v_grouped = {}
         v_packed = {}
         frame = {}
+        mean = {}
         product = {}
         attended = {}
         stationary = {}
@@ -165,12 +190,13 @@ def tile_coatten2_pb_t_kernel(tc, score_f, score_l, x_m, Wv, bv, gamma, x_f, x_l
             )
             return codes, scales
 
-        def regroup_x(i):
-            x_grouped[i] = work.tile([P, CHUNK, PACK], BF16, name="x_grouped", align_bytes=64)
-            copy = nc.vector.tensor_copy if i < VECTOR_REGROUPS else nc.scalar.copy
+        def regroup_part(i, copy, h, parts):
+            if h == 0:
+                x_grouped[i] = work.tile([P, CHUNK, PACK], BF16, name="x_grouped", align_bytes=64)
+            w = CHUNK // parts
             copy(
-                out=x_grouped[i][:].rearrange("p (c i) t -> p c t i", i=4),
-                in_=chunk_of(xm_pieces, i).rearrange("p t (c i) -> p c t i", i=4),
+                out=x_grouped[i][:, h * w : (h + 1) * w, :].rearrange("p (c i) t -> p c t i", i=4),
+                in_=xm[i][:, :, h * w : (h + 1) * w].rearrange("p t (c i) -> p c t i", i=4),
             )
 
         def project(u):
@@ -178,7 +204,7 @@ def tile_coatten2_pb_t_kernel(tc, score_f, score_l, x_m, Wv, bv, gamma, x_f, x_l
             codes, scales = x_packed[i]
             wv_codes, wv_scales = stationary["wv"]
             pixels = slice(s * SUB, (s + 1) * SUB)
-            product[u] = psum.tile([P, PACK, SUB], F32, name="product", tag="v")
+            product[u] = psum.tile([P, PACK, SUB], F32, name="product", tag="v", bufs=AHEAD)
             for t in range(PACK):
                 channels = slice(t * P, (t + 1) * P)
                 nc.tensor.matmul_mx(
@@ -202,35 +228,46 @@ def tile_coatten2_pb_t_kernel(tc, score_f, score_l, x_m, Wv, bv, gamma, x_f, x_l
                 op=ALU.add,
             )
 
-        def mean_frames(i):
+        def tensor_means(i):
+            return 3 if i < EXTRA_MEANS else 2
+
+        def begin_frame(i):
             frame[i] = frames.tile([P, PACK, CHUNK], F32, name="frame")
-            for j in range(TENSOR_MEANS):
-                mean = psum.tile([P, CHUNK], F32, name="mean", tag="m", bufs=2)
-                nc.tensor.matmul(
-                    out=mean[:], lhsT=half_identity[:], rhs=chunk_of(xl_pieces, i)[:, j, :],
-                    start=True, stop=False,
-                )
-                nc.tensor.matmul(
-                    out=mean[:], lhsT=half_identity[:], rhs=chunk_of(xf_pieces, i)[:, j, :],
-                    start=False, stop=True,
-                )
-                nc.scalar.copy(out=frame[i][:, j, :], in_=mean[:])
-            for j in range(TENSOR_MEANS, PACK):
-                nc.gpsimd.tensor_tensor(
-                    out=frame[i][:, j, :],
-                    in0=chunk_of(xl_pieces, i)[:, j, :],
-                    in1=chunk_of(xf_pieces, i)[:, j, :],
-                    op=ALU.add,
-                )
-            nc.scalar.mul(
-                out=frame[i][:, TENSOR_MEANS:, :], in_=frame[i][:, TENSOR_MEANS:, :], mul=0.5
+
+        def mean_by_tensor(i, j):
+            mean[i, j] = psum.tile([P, CHUNK], F32, name="mean", tag="m", bufs=2)
+            nc.tensor.matmul(
+                out=mean[i, j][:], lhsT=half_identity[:], rhs=xl[i][:, j, :], start=True, stop=False
             )
+            nc.tensor.matmul(
+                out=mean[i, j][:], lhsT=half_identity[:], rhs=xf[i][:, j, :], start=False, stop=True
+            )
+
+        def keep_mean(i, j):
+            nc.scalar.copy(out=frame[i][:, j, :], in_=mean[i, j][:])
+
+        def sum_by_gpsimd(i):
+            for j in range(tensor_means(i), PACK):
+                nc.gpsimd.tensor_tensor(
+                    out=frame[i][:, j, :], in0=xl[i][:, j, :], in1=xf[i][:, j, :], op=ALU.add
+                )
+
+        def halve(i):
+            first = tensor_means(i)
+            if i < GHALF:
+                for j in range(first, PACK):
+                    nc.gpsimd.tensor_scalar(
+                        out=frame[i][:, j, :], in0=frame[i][:, j, :], scalar1=0.5, scalar2=0.0,
+                        op0=ALU.mult, op1=ALU.add,
+                    )
+            else:
+                nc.scalar.mul(out=frame[i][:, first:, :], in_=frame[i][:, first:, :], mul=0.5)
 
         def attend(u):
             i, j = divmod(u, PACK)
             codes, scales = v_packed[i]
             channels = slice(j * P, (j + 1) * P)
-            attended[u] = psum.tile([P, CHUNK], F32, name="attended", tag="o")
+            attended[u] = psum.tile([P, CHUNK], F32, name="attended", tag="o", bufs=AHEAD_O)
             for which in ("f", "l"):
                 att_codes, att_scales = stationary[which]
                 nc.tensor.matmul_mx(
@@ -263,37 +300,91 @@ def tile_coatten2_pb_t_kernel(tc, score_f, score_l, x_m, Wv, bv, gamma, x_f, x_l
         def is_bank(u):
             return 0 <= u < N_BANKS
 
+        def bias_bank(u):
+            add_bias(u)
+            if is_bank(u + AHEAD):
+                project(u + AHEAD)
+
+        def frames_of(n):
+            if n < N_CHUNKS - 2:
+                return [n - 1]
+            return [n - 1, n] if n == N_CHUNKS - 2 else [n] if n == N_CHUNKS - 1 else []
+
+        waiting = []
+
         def cycle(n):
-            if is_chunk(n + 2):
-                regroup_x(n + 2)
-            if is_chunk(n - 1):
-                mean_frames(n - 1)
-            for u in range(n * PACK, (n + 1) * PACK):
+            jobs = [(i, j) for i in frames_of(n) for j in range(tensor_means(i))]
+            for i in frames_of(n):
+                begin_frame(i)
+                sum_by_gpsimd(i)
+            for s in range(PACK):
+                u = n * PACK + s
+                for job in waiting:
+                    keep_mean(*job)
+                waiting.clear()
+                if s in RSLOTS and is_chunk(n + XLEAD):
+                    regroup_part(n + XLEAD, nc.scalar.copy, RSLOTS.index(s), len(RSLOTS))
                 if is_bank(u):
-                    add_bias(u)
-                if is_bank(u + AHEAD):
-                    project(u + AHEAD)
+                    bias_bank(u)
                 if is_bank(u - LAG):
                     fuse(u - LAG)
-                if is_bank(u - LAG + AHEAD):
-                    attend(u - LAG + AHEAD)
+                for job in jobs[s::PACK]:
+                    mean_by_tensor(*job)
+                    waiting.append(job)
+                if s == 0 and is_chunk(n + 1):
+                    x_packed[n + 1] = quantise(x_grouped[n + 1], "x")
+                if is_bank(u - LAG + AHEAD_O):
+                    attend(u - LAG + AHEAD_O)
+                if s == HSLOT:
+                    for i in frames_of(n):
+                        halve(i)
             if is_chunk(n):
                 v_packed[n] = quantise(v_grouped[n], "v")
-            if is_chunk(n + 2):
-                x_packed[n + 2] = quantise(x_grouped[n + 2], "x")
 
-        e_f, sum_f = exponentials(nc, keep, score_f_rows, "f")
-        e_l, sum_l = exponentials(nc, keep, score_l_rows, "l")
-        att_f = normalise(nc, keep, e_f, sum_f, "f")
-        wv_grouped = flip_words(nc, psum, keep, identity_f32, wv_rows, "wv", nc.vector.tensor_copy)
+        def regroup(i, copy):
+            regroup_part(i, copy, 0, 1)
+
+        def pack_x(i):
+            x_packed[i] = quantise(x_grouped[i], "x")
+
+        regroup(0, nc.vector.tensor_copy)
+        wv_grouped = flip_words(nc, psum, keep, identity_f32, wv_rows, "wv", nc.scalar.copy)
+        pack_x(0)
         stationary["wv"] = quantise_matrix(nc, keep, wv_grouped, "wv")
-        att_l = normalise(nc, keep, e_l, sum_l, "l")
-        cycle(-2)
-        cycle(-1)
+        for u in range(AHEAD):
+            project(u)
+        negmax_f = row_maxima(nc, keep, score_f_rows, "f")
+        e_f, sum_f = exponentials(nc, keep, score_f_rows, negmax_f, "f")
+        regroup(1, nc.vector.tensor_copy)
+        negmax_l = row_maxima(nc, keep, score_l_rows, "l")
+        e_l, sum_l = exponentials(nc, keep, score_l_rows, negmax_l, "l")
+        pack_x(1)
+        att_f = normalise(nc, keep, e_f, sum_f, "f")
+        bias_bank(0)
+        bias_bank(1)
+        bias_bank(2)
         f_grouped = flip(nc, psum, keep, identity, att_f, "f", nc.scalar.copy)
-        cycle(0)
+        bias_bank(3)
+        begin_frame(0)
+        for j in range(tensor_means(0)):
+            mean_by_tensor(0, j)
+            keep_mean(0, j)
+        regroup(2, nc.vector.tensor_copy)
+        v_packed[0] = quantise(v_grouped[0], "v")
+        att_l = normalise(nc, keep, e_l, sum_l, "l")
+        sum_by_gpsimd(0)
+        halve(0)
+        bias_bank(4)
+        pack_x(2)
+        bias_bank(5)
         l_grouped = flip(nc, psum, keep, identity, att_l, "l", nc.scalar.copy)
+        bias_bank(6)
         stationary["f"] = quantise_matrix(nc, keep, f_grouped, "f")
+        bias_bank(7)
         stationary["l"] = quantise_matrix(nc, keep, l_grouped, "l")
-        for n in range(1, N_CHUNKS + LAG // PACK):
+        v_packed[1] = quantise(v_grouped[1], "v")
+        regroup(3, nc.scalar.copy)
+        for u in range(AHEAD_O):
+            attend(u)
+        for n in range(2, N_CHUNKS + LAG // PACK):
             cycle(n)

@@ -23,11 +23,12 @@ N_BANKS = N_CHUNKS * PACK
 AHEAD = 3
 LAG = 8
 AHEAD_O = 3
-GHALF = 5
 XLEAD = 2
-EXTRA_MEANS = 3
-RSLOTS = (0, 2)
-HSLOT = 3
+G_WIDTH = 256
+RSLOTS = (0,1,2,3)
+HSLOT = 1
+FIRST_PARTS = 1
+GNORM = ("f",)
 WORK_BUFS = 2
 
 FLOPS = 3 * 2 * C * C * PIXELS
@@ -110,10 +111,15 @@ def normalise(nc, sbuf, e, rowsum, which):
     nc.vector.reciprocal(out=inverse[:], in_=rowsum[:])
     att = sbuf.tile([P, PACK, PACK, P], BF16, name="att_" + which)
     for j in range(PACK):
-        nc.gpsimd.tensor_scalar(
-            out=att[:, j, :, :], in0=e[:, j, :, :], scalar1=inverse[:, j : j + 1], scalar2=0.0,
-            op0=ALU.mult, op1=ALU.add,
-        )
+        if which in GNORM:
+            nc.gpsimd.tensor_scalar(
+                out=att[:, j, :, :], in0=e[:, j, :, :], scalar1=inverse[:, j : j + 1], scalar2=0.0,
+                op0=ALU.mult, op1=ALU.add,
+            )
+        else:
+            nc.scalar.activation(
+                out=att[:, j, :, :], in_=e[:, j, :, :], func=ACT.Copy, scale=inverse[:, j : j + 1]
+            )
     return att
 
 
@@ -154,16 +160,13 @@ def tile_coatten2_pb_t_kernel(tc, score_f, score_l, x_m, Wv, bv, gamma, x_f, x_l
             return [piece[:, :, c * CHUNK : (c + 1) * CHUNK] for c in range(chunks)]
 
         xm = load_chunk(x_m, "xm", 0, 1)
-        wv_rows = load_matrix(Wv, "wv", 4)
         score_f_rows = load_matrix(score_f, "score_f", 2)
+        wv_rows = load_matrix(Wv, "wv", 2)
         xm += load_chunk(x_m, "xm", 1, 1)
         score_l_rows = load_matrix(score_l, "score_l", 2)
-        xm += load_chunk(x_m, "xm", 2, 1)
-        xl = load_chunk(x_l, "xl", 0, 1)
-        xf = load_chunk(x_f, "xf", 0, 1)
-        xm += load_chunk(x_m, "xm", 3, 1)
-        xl += load_chunk(x_l, "xl", 1, 1)
-        xf += load_chunk(x_f, "xf", 1, 1)
+        xm += load_chunk(x_m, "xm", 2, 2)
+        xl = load_chunk(x_l, "xl", 0, 2)
+        xf = load_chunk(x_f, "xf", 0, 2)
         for k in range(2, N_CHUNKS, 2):
             if k + 2 < N_CHUNKS:
                 xm += load_chunk(x_m, "xm", k + 2, 2)
@@ -229,7 +232,7 @@ def tile_coatten2_pb_t_kernel(tc, score_f, score_l, x_m, Wv, bv, gamma, x_f, x_l
             )
 
         def tensor_means(i):
-            return 3 if i < EXTRA_MEANS else 2
+            return 4 if i == 0 else 3 if i == 1 else 2
 
         def begin_frame(i):
             frame[i] = frames.tile([P, PACK, CHUNK], F32, name="frame")
@@ -248,20 +251,17 @@ def tile_coatten2_pb_t_kernel(tc, score_f, score_l, x_m, Wv, bv, gamma, x_f, x_l
 
         def sum_by_gpsimd(i):
             for j in range(tensor_means(i), PACK):
-                nc.gpsimd.tensor_tensor(
-                    out=frame[i][:, j, :], in0=xl[i][:, j, :], in1=xf[i][:, j, :], op=ALU.add
-                )
+                for h in range(0, CHUNK, G_WIDTH):
+                    part = slice(h, h + G_WIDTH)
+                    nc.gpsimd.tensor_tensor(
+                        out=frame[i][:, j, part], in0=xl[i][:, j, part], in1=xf[i][:, j, part], op=ALU.add
+                    )
 
         def halve(i):
             first = tensor_means(i)
-            if i < GHALF:
-                for j in range(first, PACK):
-                    nc.gpsimd.tensor_scalar(
-                        out=frame[i][:, j, :], in0=frame[i][:, j, :], scalar1=0.5, scalar2=0.0,
-                        op0=ALU.mult, op1=ALU.add,
-                    )
-            else:
-                nc.scalar.mul(out=frame[i][:, first:, :], in_=frame[i][:, first:, :], mul=0.5)
+            if first == PACK:
+                return
+            nc.scalar.mul(out=frame[i][:, first:, :], in_=frame[i][:, first:, :], mul=0.5)
 
         def attend(u):
             i, j = divmod(u, PACK)
@@ -347,14 +347,15 @@ def tile_coatten2_pb_t_kernel(tc, score_f, score_l, x_m, Wv, bv, gamma, x_f, x_l
         def pack_x(i):
             x_packed[i] = quantise(x_grouped[i], "x")
 
-        regroup(0, nc.vector.tensor_copy)
-        wv_grouped = flip_words(nc, psum, keep, identity_f32, wv_rows, "wv", nc.scalar.copy)
+        for h in range(FIRST_PARTS):
+            regroup_part(0, nc.vector.tensor_copy, h, FIRST_PARTS)
         pack_x(0)
+        negmax_f = row_maxima(nc, keep, score_f_rows, "f")
+        wv_grouped = flip_words(nc, psum, keep, identity_f32, wv_rows, "wv", nc.scalar.copy)
+        e_f, sum_f = exponentials(nc, keep, score_f_rows, negmax_f, "f")
         stationary["wv"] = quantise_matrix(nc, keep, wv_grouped, "wv")
         for u in range(AHEAD):
             project(u)
-        negmax_f = row_maxima(nc, keep, score_f_rows, "f")
-        e_f, sum_f = exponentials(nc, keep, score_f_rows, negmax_f, "f")
         regroup(1, nc.vector.tensor_copy)
         negmax_l = row_maxima(nc, keep, score_l_rows, "l")
         e_l, sum_l = exponentials(nc, keep, score_l_rows, negmax_l, "l")
@@ -363,28 +364,32 @@ def tile_coatten2_pb_t_kernel(tc, score_f, score_l, x_m, Wv, bv, gamma, x_f, x_l
         bias_bank(0)
         bias_bank(1)
         bias_bank(2)
-        f_grouped = flip(nc, psum, keep, identity, att_f, "f", nc.scalar.copy)
         bias_bank(3)
-        begin_frame(0)
-        for j in range(tensor_means(0)):
-            mean_by_tensor(0, j)
-            keep_mean(0, j)
+        att_l = normalise(nc, keep, e_l, sum_l, "l")
+        bias_bank(4)
+        f_grouped = flip(nc, psum, keep, identity, att_f, "f", nc.scalar.copy)
+        l_grouped = flip(nc, psum, keep, identity, att_l, "l", nc.scalar.copy)
         regroup(2, nc.vector.tensor_copy)
         v_packed[0] = quantise(v_grouped[0], "v")
-        att_l = normalise(nc, keep, e_l, sum_l, "l")
+        pack_x(2)
+        begin_frame(0)
         sum_by_gpsimd(0)
         halve(0)
-        bias_bank(4)
-        pack_x(2)
-        bias_bank(5)
-        l_grouped = flip(nc, psum, keep, identity, att_l, "l", nc.scalar.copy)
-        bias_bank(6)
-        stationary["f"] = quantise_matrix(nc, keep, f_grouped, "f")
-        bias_bank(7)
-        stationary["l"] = quantise_matrix(nc, keep, l_grouped, "l")
-        v_packed[1] = quantise(v_grouped[1], "v")
         regroup(3, nc.scalar.copy)
+        mean_by_tensor(0, 0)
+        mean_by_tensor(0, 1)
+        bias_bank(5)
+        stationary["f"] = quantise_matrix(nc, keep, f_grouped, "f")
+        stationary["l"] = quantise_matrix(nc, keep, l_grouped, "l")
         for u in range(AHEAD_O):
             attend(u)
+        keep_mean(0, 0)
+        keep_mean(0, 1)
+        bias_bank(6)
+        for j in range(2, tensor_means(0)):
+            mean_by_tensor(0, j)
+            keep_mean(0, j)
+        bias_bank(7)
+        v_packed[1] = quantise(v_grouped[1], "v")
         for n in range(2, N_CHUNKS + LAG // PACK):
             cycle(n)

@@ -24,9 +24,9 @@ AHEAD = 3
 LAG = 8
 AHEAD_O = 3
 XLEAD = 2
-G_WIDTH = 256
 RSLOTS = (0,1,2,3)
-HSLOT = 1
+HSLOT = 2
+QSLOT = 0
 FIRST_PARTS = 1
 GNORM = ("f",)
 WORK_BUFS = 2
@@ -250,12 +250,10 @@ def tile_coatten2_pb_t_kernel(tc, score_f, score_l, x_m, Wv, bv, gamma, x_f, x_l
             nc.scalar.copy(out=frame[i][:, j, :], in_=mean[i, j][:])
 
         def sum_by_gpsimd(i):
-            for j in range(tensor_means(i), PACK):
-                for h in range(0, CHUNK, G_WIDTH):
-                    part = slice(h, h + G_WIDTH)
-                    nc.gpsimd.tensor_tensor(
-                        out=frame[i][:, j, part], in0=xl[i][:, j, part], in1=xf[i][:, j, part], op=ALU.add
-                    )
+            for j in reversed(range(tensor_means(i), PACK)):
+                nc.gpsimd.tensor_tensor(
+                    out=frame[i][:, j, :], in0=xl[i][:, j, :], in1=xf[i][:, j, :], op=ALU.add
+                )
 
         def halve(i):
             first = tensor_means(i)
@@ -316,7 +314,6 @@ def tile_coatten2_pb_t_kernel(tc, score_f, score_l, x_m, Wv, bv, gamma, x_f, x_l
             jobs = [(i, j) for i in frames_of(n) for j in range(tensor_means(i))]
             for i in frames_of(n):
                 begin_frame(i)
-                sum_by_gpsimd(i)
             for s in range(PACK):
                 u = n * PACK + s
                 for job in waiting:
@@ -331,16 +328,20 @@ def tile_coatten2_pb_t_kernel(tc, score_f, score_l, x_m, Wv, bv, gamma, x_f, x_l
                 for job in jobs[s::PACK]:
                     mean_by_tensor(*job)
                     waiting.append(job)
-                if s == 0 and is_chunk(n + 1):
-                    x_packed[n + 1] = quantise(x_grouped[n + 1], "x")
+                if s == QSLOT:
+                    if is_chunk(n - 1):
+                        v_packed[n - 1] = quantise(v_grouped[n - 1], "v")
+                    if is_chunk(n + 1):
+                        x_packed[n + 1] = quantise(x_grouped[n + 1], "x")
+                    for i in frames_of(n):
+                        if is_chunk(n):
+                            nc.vector.memset(frame[i][:, PACK - 1, 0:1], 0.0)
+                        sum_by_gpsimd(i)
                 if is_bank(u - LAG + AHEAD_O):
                     attend(u - LAG + AHEAD_O)
                 if s == HSLOT:
                     for i in frames_of(n):
                         halve(i)
-            if is_chunk(n):
-                v_packed[n] = quantise(v_grouped[n], "v")
-
         def regroup(i, copy):
             regroup_part(i, copy, 0, 1)
 
@@ -390,6 +391,5 @@ def tile_coatten2_pb_t_kernel(tc, score_f, score_l, x_m, Wv, bv, gamma, x_f, x_l
             mean_by_tensor(0, j)
             keep_mean(0, j)
         bias_bank(7)
-        v_packed[1] = quantise(v_grouped[1], "v")
         for n in range(2, N_CHUNKS + LAG // PACK):
             cycle(n)

@@ -24,11 +24,11 @@ AHEAD = 3
 LAG = 8
 AHEAD_O = 3
 XLEAD = 2
-RSLOTS = (0,1,2,3)
-HSLOT = 2
+RSLOTS = (0, 1)
+HSLOT = 0
 QSLOT = 0
-FIRST_PARTS = 1
 GNORM = ("f",)
+LATE = 3
 WORK_BUFS = 2
 
 FLOPS = 3 * 2 * C * C * PIXELS
@@ -73,13 +73,13 @@ def row_maxima(nc, sbuf, score, which):
     halves = []
     quarters = []
     for k, pair in enumerate(pairs):
-        half = sbuf.tile([P, 2, C // 2], BF16, name="half_%s%d" % (which, k))
+        half = sbuf.tile([P, 2, C // 2], BF16, name="half_%d" % k)
         nc.vector.tensor_tensor(
             out=half[:], in0=score[:, pair, : C // 2], in1=score[:, pair, C // 2 :], op=ALU.max
         )
         halves.append(half)
     for k, half in enumerate(halves):
-        quarter = sbuf.tile([P, 2, C // 4], BF16, name="quarter_%s%d" % (which, k))
+        quarter = sbuf.tile([P, 2, C // 4], BF16, name="quarter_%d" % k)
         nc.vector.tensor_tensor(
             out=quarter[:], in0=half[:, :, : C // 4], in1=half[:, :, C // 4 :], op=ALU.max
         )
@@ -146,6 +146,9 @@ def tile_coatten2_pb_t_kernel(tc, score_f, score_l, x_m, Wv, bv, gamma, x_f, x_l
         nc.scalar.dma_start(out=bias[:], in_=bv.rearrange("(p t) -> p t", t=PACK))
         gain = keep.tile([P, 1], BF16, name="gain")
         nc.scalar.dma_start(out=gain[:], in_=gamma.partition_broadcast(P))
+
+        gain_f32 = keep.tile([P, 1], F32, name="gain_f32")
+        nc.gpsimd.tensor_copy(out=gain_f32[:], in_=gain[:])
 
         def load_matrix(matrix, which, parts):
             rows = keep.tile([P, PACK, C], BF16, name=which + "_rows")
@@ -232,7 +235,7 @@ def tile_coatten2_pb_t_kernel(tc, score_f, score_l, x_m, Wv, bv, gamma, x_f, x_l
             )
 
         def tensor_means(i):
-            return 4 if i == 0 else 3 if i == 1 else 2
+            return 3 if i < 3 else 2
 
         def begin_frame(i):
             frame[i] = frames.tile([P, PACK, CHUNK], F32, name="frame")
@@ -261,6 +264,13 @@ def tile_coatten2_pb_t_kernel(tc, score_f, score_l, x_m, Wv, bv, gamma, x_f, x_l
                 return
             nc.scalar.mul(out=frame[i][:, first:, :], in_=frame[i][:, first:, :], mul=0.5)
 
+        def halve_by_gpsimd(i):
+            first = tensor_means(i)
+            nc.gpsimd.tensor_scalar(
+                out=frame[i][:, first:, :], in0=frame[i][:, first:, :], scalar1=0.5, scalar2=0.0,
+                op0=ALU.mult, op1=ALU.add,
+            )
+
         def attend(u):
             i, j = divmod(u, PACK)
             codes, scales = v_packed[i]
@@ -278,19 +288,49 @@ def tile_coatten2_pb_t_kernel(tc, score_f, score_l, x_m, Wv, bv, gamma, x_f, x_l
                     stop=(which == "l"),
                 )
 
+        def by_scalar(u):
+            i, j = divmod(u, PACK)
+            return j == 1 and i <= 3
+
+        scaled = {}
+
+        def fuse_s(u):
+            if by_scalar(u):
+                scaled[u] = work.tile([P, CHUNK], F32, name="scaled")
+                nc.scalar.activation(out=scaled[u][:], in_=attended[u][:], func=ACT.Copy, scale=gain_f32[:, 0:1])
+
         def fuse(u):
             i, j = divmod(u, PACK)
-            nc.vector.scalar_tensor_tensor(
-                out=frame[i][:, j, :],
-                in0=attended[u][:],
-                scalar=gain[:, 0:1],
-                in1=frame[i][:, j, :],
-                op0=ALU.mult,
-                op1=ALU.add,
-            )
+            if by_scalar(u):
+                nc.gpsimd.tensor_tensor(
+                    out=frame[i][:, j, :], in0=scaled[u][:], in1=frame[i][:, j, :], op=ALU.add
+                )
+            else:
+                nc.vector.scalar_tensor_tensor(
+                    out=frame[i][:, j, :],
+                    in0=attended[u][:],
+                    scalar=gain[:, 0:1],
+                    in1=frame[i][:, j, :],
+                    op0=ALU.mult,
+                    op1=ALU.add,
+                )
+            if by_scalar(u):
+                late.append(u)
+            else:
+                store(u)
+
+        late = []
+
+        def store(u):
+            i, j = divmod(u, PACK)
             nc.sync.dma_start(
                 out=by_rows(out)[:, j, i * CHUNK : (i + 1) * CHUNK], in_=frame[i][:, j, :]
             )
+
+        def store_late(u):
+            for v in [v for v in late if v <= u]:
+                store(v)
+                late.remove(v)
 
         def is_chunk(i):
             return 0 <= i < N_CHUNKS
@@ -316,6 +356,8 @@ def tile_coatten2_pb_t_kernel(tc, score_f, score_l, x_m, Wv, bv, gamma, x_f, x_l
                 begin_frame(i)
             for s in range(PACK):
                 u = n * PACK + s
+                if is_bank(u - LAG):
+                    fuse_s(u - LAG)
                 for job in waiting:
                     keep_mean(*job)
                 waiting.clear()
@@ -325,6 +367,7 @@ def tile_coatten2_pb_t_kernel(tc, score_f, score_l, x_m, Wv, bv, gamma, x_f, x_l
                     bias_bank(u)
                 if is_bank(u - LAG):
                     fuse(u - LAG)
+                    store_late(u - LAG - LATE)
                 for job in jobs[s::PACK]:
                     mean_by_tensor(*job)
                     waiting.append(job)
@@ -333,23 +376,23 @@ def tile_coatten2_pb_t_kernel(tc, score_f, score_l, x_m, Wv, bv, gamma, x_f, x_l
                         v_packed[n - 1] = quantise(v_grouped[n - 1], "v")
                     if is_chunk(n + 1):
                         x_packed[n + 1] = quantise(x_grouped[n + 1], "x")
-                    for i in frames_of(n):
-                        if is_chunk(n):
+                    for k, i in enumerate(frames_of(n)):
+                        if k == 0:
                             nc.vector.memset(frame[i][:, PACK - 1, 0:1], 0.0)
                         sum_by_gpsimd(i)
                 if is_bank(u - LAG + AHEAD_O):
                     attend(u - LAG + AHEAD_O)
                 if s == HSLOT:
-                    for i in frames_of(n):
+                    for i in frames_of(n - 1) if n > 2 else []:
                         halve(i)
+
         def regroup(i, copy):
             regroup_part(i, copy, 0, 1)
 
         def pack_x(i):
             x_packed[i] = quantise(x_grouped[i], "x")
 
-        for h in range(FIRST_PARTS):
-            regroup_part(0, nc.vector.tensor_copy, h, FIRST_PARTS)
+        regroup(0, nc.vector.tensor_copy)
         pack_x(0)
         negmax_f = row_maxima(nc, keep, score_f_rows, "f")
         wv_grouped = flip_words(nc, psum, keep, identity_f32, wv_rows, "wv", nc.scalar.copy)
@@ -362,34 +405,36 @@ def tile_coatten2_pb_t_kernel(tc, score_f, score_l, x_m, Wv, bv, gamma, x_f, x_l
         e_l, sum_l = exponentials(nc, keep, score_l_rows, negmax_l, "l")
         pack_x(1)
         att_f = normalise(nc, keep, e_f, sum_f, "f")
-        bias_bank(0)
-        bias_bank(1)
-        bias_bank(2)
-        bias_bank(3)
-        att_l = normalise(nc, keep, e_l, sum_l, "l")
-        bias_bank(4)
-        f_grouped = flip(nc, psum, keep, identity, att_f, "f", nc.scalar.copy)
-        l_grouped = flip(nc, psum, keep, identity, att_l, "l", nc.scalar.copy)
-        regroup(2, nc.vector.tensor_copy)
-        v_packed[0] = quantise(v_grouped[0], "v")
-        pack_x(2)
         begin_frame(0)
         sum_by_gpsimd(0)
-        halve(0)
-        regroup(3, nc.scalar.copy)
+        halve_by_gpsimd(0)
+        for u in range(PACK - 1):
+            bias_bank(u)
+        att_l = normalise(nc, keep, e_l, sum_l, "l")
+        bias_bank(PACK - 1)
+        for u in range(PACK, 2 * PACK - AHEAD):
+            bias_bank(u)
+        f_grouped = flip(nc, psum, keep, identity, att_f, "f", nc.scalar.copy)
+        for u in range(2 * PACK - AHEAD, 2 * PACK):
+            add_bias(u)
+        v_packed[0] = quantise(v_grouped[0], "v")
+        regroup(2, nc.vector.tensor_copy)
+        pack_x(2)
+        l_grouped = flip(nc, psum, keep, identity, att_l, "l", nc.scalar.copy)
         mean_by_tensor(0, 0)
         mean_by_tensor(0, 1)
-        bias_bank(5)
+        keep_mean(0, 0)
+        keep_mean(0, 1)
+        for u in range(2 * PACK, 2 * PACK + AHEAD):
+            project(u)
         stationary["f"] = quantise_matrix(nc, keep, f_grouped, "f")
         stationary["l"] = quantise_matrix(nc, keep, l_grouped, "l")
         for u in range(AHEAD_O):
             attend(u)
-        keep_mean(0, 0)
-        keep_mean(0, 1)
-        bias_bank(6)
+        regroup(3, nc.scalar.copy)
         for j in range(2, tensor_means(0)):
             mean_by_tensor(0, j)
             keep_mean(0, j)
-        bias_bank(7)
         for n in range(2, N_CHUNKS + LAG // PACK):
             cycle(n)
+        store_late(N_BANKS)

@@ -29,6 +29,7 @@ HSLOT = 0
 QSLOT = 0
 GNORM = ("f",)
 LATE = 3
+T_MOST = 3
 WORK_BUFS = 2
 
 FLOPS = 3 * 2 * C * C * PIXELS
@@ -162,11 +163,11 @@ def tile_coatten2_pb_t_kernel(tc, score_f, score_l, x_m, Wv, bv, gamma, x_f, x_l
             nc.sync.dma_start(out=piece[:], in_=by_rows(matrix)[:, :, k * CHUNK : (k + chunks) * CHUNK])
             return [piece[:, :, c * CHUNK : (c + 1) * CHUNK] for c in range(chunks)]
 
-        xm = load_chunk(x_m, "xm", 0, 1)
         score_f_rows = load_matrix(score_f, "score_f", 2)
+        xm = load_chunk(x_m, "xm", 0, 1)
         wv_rows = load_matrix(Wv, "wv", 2)
-        xm += load_chunk(x_m, "xm", 1, 1)
         score_l_rows = load_matrix(score_l, "score_l", 2)
+        xm += load_chunk(x_m, "xm", 1, 1)
         xm += load_chunk(x_m, "xm", 2, 2)
         xl = load_chunk(x_l, "xl", 0, 2)
         xf = load_chunk(x_f, "xf", 0, 2)
@@ -238,7 +239,8 @@ def tile_coatten2_pb_t_kernel(tc, score_f, score_l, x_m, Wv, bv, gamma, x_f, x_l
             return 3 if i < 3 else 2
 
         def begin_frame(i):
-            frame[i] = frames.tile([P, PACK, CHUNK], F32, name="frame")
+            if i not in frame:
+                frame[i] = frames.tile([P, PACK, CHUNK], F32, name="frame")
 
         def mean_by_tensor(i, j):
             mean[i, j] = psum.tile([P, CHUNK], F32, name="mean", tag="m", bufs=2)
@@ -252,22 +254,17 @@ def tile_coatten2_pb_t_kernel(tc, score_f, score_l, x_m, Wv, bv, gamma, x_f, x_l
         def keep_mean(i, j):
             nc.scalar.copy(out=frame[i][:, j, :], in_=mean[i, j][:])
 
-        def sum_by_gpsimd(i):
-            for j in reversed(range(tensor_means(i), PACK)):
-                nc.gpsimd.tensor_tensor(
-                    out=frame[i][:, j, :], in0=xl[i][:, j, :], in1=xf[i][:, j, :], op=ALU.add
-                )
+        def sum_by_gpsimd(i, j):
+            nc.gpsimd.tensor_tensor(
+                out=frame[i][:, j, :], in0=xl[i][:, j, :], in1=xf[i][:, j, :], op=ALU.add
+            )
 
-        def halve(i):
-            first = tensor_means(i)
-            if first == PACK:
-                return
-            nc.scalar.mul(out=frame[i][:, first:, :], in_=frame[i][:, first:, :], mul=0.5)
+        def halve(i, j):
+            nc.scalar.mul(out=frame[i][:, j, :], in_=frame[i][:, j, :], mul=0.5)
 
-        def halve_by_gpsimd(i):
-            first = tensor_means(i)
+        def halve_by_gpsimd(i, j):
             nc.gpsimd.tensor_scalar(
-                out=frame[i][:, first:, :], in0=frame[i][:, first:, :], scalar1=0.5, scalar2=0.0,
+                out=frame[i][:, j, :], in0=frame[i][:, j, :], scalar1=0.5, scalar2=0.0,
                 op0=ALU.mult, op1=ALU.add,
             )
 
@@ -290,7 +287,7 @@ def tile_coatten2_pb_t_kernel(tc, score_f, score_l, x_m, Wv, bv, gamma, x_f, x_l
 
         def by_scalar(u):
             i, j = divmod(u, PACK)
-            return j == 1 and i <= 3
+            return j == 1 and i <= 5
 
         scaled = {}
 
@@ -343,17 +340,24 @@ def tile_coatten2_pb_t_kernel(tc, score_f, score_l, x_m, Wv, bv, gamma, x_f, x_l
             if is_bank(u + AHEAD):
                 project(u + AHEAD)
 
-        def frames_of(n):
-            if n < N_CHUNKS - 2:
-                return [n - 1]
-            return [n - 1, n] if n == N_CHUNKS - 2 else [n] if n == N_CHUNKS - 1 else []
-
         waiting = []
+        summed = []
+        tensor_jobs = [(i, j) for i in range(1, N_CHUNKS) for j in range(tensor_means(i))]
+        gpsimd_jobs = [(i, j) for i in range(1, N_CHUNKS) for j in range(tensor_means(i), PACK)]
+
+        def take(jobs, most, last_chunk):
+            taken = [job for job in jobs[:most] if job[0] <= last_chunk]
+            for job in taken:
+                jobs.remove(job)
+                begin_frame(job[0])
+            return taken
 
         def cycle(n):
-            jobs = [(i, j) for i in frames_of(n) for j in range(tensor_means(i))]
-            for i in frames_of(n):
-                begin_frame(i)
+            means = take(tensor_jobs, T_MOST, n if n >= N_CHUNKS - 2 else n - 1)
+            sums = take(gpsimd_jobs, 2, n if n > 2 else n - 1)
+            halves = list(summed)
+            summed.clear()
+            summed.extend(sums)
             for s in range(PACK):
                 u = n * PACK + s
                 if is_bank(u - LAG):
@@ -368,7 +372,7 @@ def tile_coatten2_pb_t_kernel(tc, score_f, score_l, x_m, Wv, bv, gamma, x_f, x_l
                 if is_bank(u - LAG):
                     fuse(u - LAG)
                     store_late(u - LAG - LATE)
-                for job in jobs[s::PACK]:
+                for job in means[s::PACK]:
                     mean_by_tensor(*job)
                     waiting.append(job)
                 if s == QSLOT:
@@ -376,15 +380,16 @@ def tile_coatten2_pb_t_kernel(tc, score_f, score_l, x_m, Wv, bv, gamma, x_f, x_l
                         v_packed[n - 1] = quantise(v_grouped[n - 1], "v")
                     if is_chunk(n + 1):
                         x_packed[n + 1] = quantise(x_grouped[n + 1], "x")
-                    for k, i in enumerate(frames_of(n)):
-                        if k == 0:
-                            nc.vector.memset(frame[i][:, PACK - 1, 0:1], 0.0)
-                        sum_by_gpsimd(i)
+                    if sums:
+                        i, j = sums[0]
+                        nc.vector.memset(frame[i][:, j, 0:1], 0.0)
+                    for job in sums:
+                        sum_by_gpsimd(*job)
                 if is_bank(u - LAG + AHEAD_O):
                     attend(u - LAG + AHEAD_O)
                 if s == HSLOT:
-                    for i in frames_of(n - 1) if n > 2 else []:
-                        halve(i)
+                    for job in halves:
+                        halve(*job)
 
         def regroup(i, copy):
             regroup_part(i, copy, 0, 1)
@@ -392,33 +397,33 @@ def tile_coatten2_pb_t_kernel(tc, score_f, score_l, x_m, Wv, bv, gamma, x_f, x_l
         def pack_x(i):
             x_packed[i] = quantise(x_grouped[i], "x")
 
+        negmax_f = row_maxima(nc, keep, score_f_rows, "f")
+        e_f, sum_f = exponentials(nc, keep, score_f_rows, negmax_f, "f")
         regroup(0, nc.vector.tensor_copy)
         pack_x(0)
-        negmax_f = row_maxima(nc, keep, score_f_rows, "f")
         wv_grouped = flip_words(nc, psum, keep, identity_f32, wv_rows, "wv", nc.scalar.copy)
-        e_f, sum_f = exponentials(nc, keep, score_f_rows, negmax_f, "f")
+        negmax_l = row_maxima(nc, keep, score_l_rows, "l")
+        e_l, sum_l = exponentials(nc, keep, score_l_rows, negmax_l, "l")
+        regroup(1, nc.vector.tensor_copy)
         stationary["wv"] = quantise_matrix(nc, keep, wv_grouped, "wv")
         for u in range(AHEAD):
             project(u)
-        regroup(1, nc.vector.tensor_copy)
-        negmax_l = row_maxima(nc, keep, score_l_rows, "l")
-        e_l, sum_l = exponentials(nc, keep, score_l_rows, negmax_l, "l")
         pack_x(1)
         att_f = normalise(nc, keep, e_f, sum_f, "f")
         begin_frame(0)
-        sum_by_gpsimd(0)
-        halve_by_gpsimd(0)
-        for u in range(PACK - 1):
-            bias_bank(u)
+        for j in range(tensor_means(0), PACK):
+            sum_by_gpsimd(0, j)
+            halve_by_gpsimd(0, j)
+        bias_bank(0)
         att_l = normalise(nc, keep, e_l, sum_l, "l")
-        bias_bank(PACK - 1)
-        for u in range(PACK, 2 * PACK - AHEAD):
+        regroup_part(2, nc.scalar.copy, 0, 2)
+        for u in range(1, 2 * PACK - AHEAD):
             bias_bank(u)
         f_grouped = flip(nc, psum, keep, identity, att_f, "f", nc.scalar.copy)
         for u in range(2 * PACK - AHEAD, 2 * PACK):
             add_bias(u)
         v_packed[0] = quantise(v_grouped[0], "v")
-        regroup(2, nc.vector.tensor_copy)
+        regroup_part(2, nc.vector.tensor_copy, 1, 2)
         pack_x(2)
         l_grouped = flip(nc, psum, keep, identity, att_l, "l", nc.scalar.copy)
         mean_by_tensor(0, 0)

@@ -30,6 +30,8 @@ QSLOT = 0
 GNORM = ("f",)
 LATE = 3
 T_MOST = 3
+QUAD = 4
+GROUPS = ((0, 3), (4, 5), (6, 6), (7, 7))
 WORK_BUFS = 2
 
 FLOPS = 3 * 2 * C * C * PIXELS
@@ -92,8 +94,8 @@ def row_maxima(nc, sbuf, score, which):
     return negmax
 
 
-def exponentials(nc, sbuf, score, negmax, which):
-    e = sbuf.tile([P, PACK, PACK, P], F32, name="e_" + which)
+def exponentials(nc, sbuf, early, score, negmax, which):
+    e = early.tile([P, PACK, PACK, P], F32, name="e_" + which, tag="early")
     rowsum = sbuf.tile([P, PACK], F32, name="rowsum_" + which)
     for j in range(PACK):
         nc.scalar.activation(
@@ -129,8 +131,8 @@ def tile_coatten2_pb_t_kernel(tc, score_f, score_l, x_m, Wv, bv, gamma, x_f, x_l
     with ExitStack() as stack:
         stack.enter_context(tc.manual_schedule())
         keep = stack.enter_context(tc.tile_pool(name="keep", bufs=1))
+        early = stack.enter_context(tc.tile_pool(name="early", bufs=2))
         work = stack.enter_context(tc.tile_pool(name="work", bufs=WORK_BUFS))
-        frames = stack.enter_context(tc.tile_pool(name="frames", bufs=6))
         psum = stack.enter_context(tc.psum_pool(name="psum", bufs=2))
 
         identity_f32 = keep.tile([P, P], F32, name="identity_f32")
@@ -145,11 +147,11 @@ def tile_coatten2_pb_t_kernel(tc, score_f, score_l, x_m, Wv, bv, gamma, x_f, x_l
 
         bias = keep.tile([P, PACK], BF16, name="bias")
         nc.scalar.dma_start(out=bias[:], in_=bv.rearrange("(p t) -> p t", t=PACK))
-        gain = keep.tile([P, 1], BF16, name="gain")
-        nc.scalar.dma_start(out=gain[:], in_=gamma.partition_broadcast(P))
-
-        gain_f32 = keep.tile([P, 1], F32, name="gain_f32")
-        nc.gpsimd.tensor_copy(out=gain_f32[:], in_=gain[:])
+        gain_row = keep.tile([P, 2], BF16, name="gain_row")
+        nc.gpsimd.memset(gain_row[:], 0.0)
+        ones = keep.tile([P, P], BF16, name="ones")
+        nc.gpsimd.memset(ones[:], 1.0)
+        gain = keep.tile([P, 1], F32, name="gain")
 
         def load_matrix(matrix, which, parts):
             rows = keep.tile([P, PACK, C], BF16, name=which + "_rows")
@@ -158,22 +160,22 @@ def tile_coatten2_pb_t_kernel(tc, score_f, score_l, x_m, Wv, bv, gamma, x_f, x_l
                 nc.sync.dma_start(out=rows[:, part, :], in_=by_rows(matrix)[:, part, :])
             return rows
 
-        def load_chunk(matrix, which, k, chunks):
-            piece = keep.tile([P, PACK, chunks * CHUNK], BF16, name="%s_%d" % (which, k))
+        def load_chunk(matrix, which, k, chunks, pool=keep):
+            piece = pool.tile([P, PACK, chunks * CHUNK], BF16, name="%s_%d" % (which, k), tag="%s_%d" % (which, k) if pool is keep else "early")
             nc.sync.dma_start(out=piece[:], in_=by_rows(matrix)[:, :, k * CHUNK : (k + chunks) * CHUNK])
             return [piece[:, :, c * CHUNK : (c + 1) * CHUNK] for c in range(chunks)]
 
         score_f_rows = load_matrix(score_f, "score_f", 2)
         xm = load_chunk(x_m, "xm", 0, 1)
-        wv_rows = load_matrix(Wv, "wv", 2)
         score_l_rows = load_matrix(score_l, "score_l", 2)
+        wv_rows = load_matrix(Wv, "wv", 1)
         xm += load_chunk(x_m, "xm", 1, 1)
+        nc.sync.dma_start(out=gain_row[0:1, 0:1], in_=gamma.unsqueeze(0))
         xm += load_chunk(x_m, "xm", 2, 2)
         xl = load_chunk(x_l, "xl", 0, 2)
         xf = load_chunk(x_f, "xf", 0, 2)
-        for k in range(2, N_CHUNKS, 2):
-            if k + 2 < N_CHUNKS:
-                xm += load_chunk(x_m, "xm", k + 2, 2)
+        for k in range(2, N_CHUNKS - 2, 2):
+            xm += load_chunk(x_m, "xm", k + 2, 2)
             xl += load_chunk(x_l, "xl", k, 2)
             xf += load_chunk(x_f, "xf", k, 2)
 
@@ -182,6 +184,7 @@ def tile_coatten2_pb_t_kernel(tc, score_f, score_l, x_m, Wv, bv, gamma, x_f, x_l
         v_grouped = {}
         v_packed = {}
         frame = {}
+        quads = {}
         mean = {}
         product = {}
         attended = {}
@@ -239,8 +242,10 @@ def tile_coatten2_pb_t_kernel(tc, score_f, score_l, x_m, Wv, bv, gamma, x_f, x_l
             return 3 if i < 3 else 2
 
         def begin_frame(i):
-            if i not in frame:
-                frame[i] = frames.tile([P, PACK, CHUNK], F32, name="frame")
+            k = i // QUAD
+            if k not in quads:
+                quads[k] = keep.tile([P, PACK, QUAD * CHUNK], F32, name="frames_%d" % k)
+            frame[i] = quads[k][:, :, (i % QUAD) * CHUNK : (i % QUAD + 1) * CHUNK]
 
         def mean_by_tensor(i, j):
             mean[i, j] = psum.tile([P, CHUNK], F32, name="mean", tag="m", bufs=2)
@@ -294,7 +299,7 @@ def tile_coatten2_pb_t_kernel(tc, score_f, score_l, x_m, Wv, bv, gamma, x_f, x_l
         def fuse_s(u):
             if by_scalar(u):
                 scaled[u] = work.tile([P, CHUNK], F32, name="scaled")
-                nc.scalar.activation(out=scaled[u][:], in_=attended[u][:], func=ACT.Copy, scale=gain_f32[:, 0:1])
+                nc.scalar.activation(out=scaled[u][:], in_=attended[u][:], func=ACT.Copy, scale=gain[:, 0:1])
 
         def fuse(u):
             i, j = divmod(u, PACK)
@@ -320,9 +325,13 @@ def tile_coatten2_pb_t_kernel(tc, score_f, score_l, x_m, Wv, bv, gamma, x_f, x_l
 
         def store(u):
             i, j = divmod(u, PACK)
-            nc.sync.dma_start(
-                out=by_rows(out)[:, j, i * CHUNK : (i + 1) * CHUNK], in_=frame[i][:, j, :]
-            )
+            for first, last in GROUPS:
+                if i == last:
+                    k = first % QUAD
+                    nc.sync.dma_start(
+                        out=by_rows(out)[:, j, first * CHUNK : (last + 1) * CHUNK],
+                        in_=quads[i // QUAD][:, j, k * CHUNK : (k + last - first + 1) * CHUNK],
+                    )
 
         def store_late(u):
             for v in [v for v in late if v <= u]:
@@ -398,12 +407,12 @@ def tile_coatten2_pb_t_kernel(tc, score_f, score_l, x_m, Wv, bv, gamma, x_f, x_l
             x_packed[i] = quantise(x_grouped[i], "x")
 
         negmax_f = row_maxima(nc, keep, score_f_rows, "f")
-        e_f, sum_f = exponentials(nc, keep, score_f_rows, negmax_f, "f")
+        e_f, sum_f = exponentials(nc, keep, early, score_f_rows, negmax_f, "f")
         regroup(0, nc.vector.tensor_copy)
         pack_x(0)
         wv_grouped = flip_words(nc, psum, keep, identity_f32, wv_rows, "wv", nc.scalar.copy)
         negmax_l = row_maxima(nc, keep, score_l_rows, "l")
-        e_l, sum_l = exponentials(nc, keep, score_l_rows, negmax_l, "l")
+        e_l, sum_l = exponentials(nc, keep, early, score_l_rows, negmax_l, "l")
         regroup(1, nc.vector.tensor_copy)
         stationary["wv"] = quantise_matrix(nc, keep, wv_grouped, "wv")
         for u in range(AHEAD):
@@ -419,6 +428,9 @@ def tile_coatten2_pb_t_kernel(tc, score_f, score_l, x_m, Wv, bv, gamma, x_f, x_l
         regroup_part(2, nc.scalar.copy, 0, 2)
         for u in range(1, 2 * PACK - AHEAD):
             bias_bank(u)
+        spread = psum.tile([P, 2], F32, name="spread", tag="m", bufs=2)
+        nc.tensor.matmul(out=spread[:], lhsT=ones[:], rhs=gain_row[:], start=True, stop=True)
+        nc.scalar.copy(out=gain[:], in_=spread[:, 0:1])
         f_grouped = flip(nc, psum, keep, identity, att_f, "f", nc.scalar.copy)
         for u in range(2 * PACK - AHEAD, 2 * PACK):
             add_bias(u)
@@ -440,6 +452,8 @@ def tile_coatten2_pb_t_kernel(tc, score_f, score_l, x_m, Wv, bv, gamma, x_f, x_l
         for j in range(2, tensor_means(0)):
             mean_by_tensor(0, j)
             keep_mean(0, j)
+        xl += load_chunk(x_l, "xl", N_CHUNKS - 2, 2, early)
+        xf += load_chunk(x_f, "xf", N_CHUNKS - 2, 2, early)
         for n in range(2, N_CHUNKS + LAG // PACK):
             cycle(n)
         store_late(N_BANKS)

@@ -167,7 +167,7 @@ def tile_coatten2_pb_t_kernel(tc, score_f, score_l, x_m, Wv, bv, gamma, x_f, x_l
 
         score_f_rows = load_matrix(score_f, "score_f", 2)
         xm = load_chunk(x_m, "xm", 0, 1)
-        score_l_rows = load_matrix(score_l, "score_l", 2)
+        score_l_rows = load_matrix(score_l, "score_l", 1)
         wv_rows = load_matrix(Wv, "wv", 1)
         xm += load_chunk(x_m, "xm", 1, 1)
         nc.sync.dma_start(out=gain_row[0:1, 0:1], in_=gamma.unsqueeze(0))
@@ -239,7 +239,7 @@ def tile_coatten2_pb_t_kernel(tc, score_f, score_l, x_m, Wv, bv, gamma, x_f, x_l
             )
 
         def tensor_means(i):
-            return 3 if i < 3 else 2
+            return 3 if i == 0 else 2
 
         def begin_frame(i):
             k = i // QUAD
@@ -292,7 +292,7 @@ def tile_coatten2_pb_t_kernel(tc, score_f, score_l, x_m, Wv, bv, gamma, x_f, x_l
 
         def by_scalar(u):
             i, j = divmod(u, PACK)
-            return j == 1 and i <= 5
+            return j == 1 and i <= 4
 
         scaled = {}
 

from contextlib import ExitStack

import concourse.mybir as mybir
from concourse.masks import make_identity

BF16 = mybir.dt.bfloat16
F32 = mybir.dt.float32
U32 = mybir.dt.uint32
U8 = mybir.dt.uint8
FP8X4 = mybir.dt.float8_e4m3fn_x4
ALU = mybir.AluOpType
ACT = mybir.ActivationFunctionType
AXIS = mybir.AxisListType

P = 128
PACK = 4
C = P * PACK
PIXELS = 4096
CHUNK = 512
N_CHUNKS = PIXELS // CHUNK
SUB = CHUNK // PACK
N_BANKS = N_CHUNKS * PACK
AHEAD = 3
LAG = 8
AHEAD_O = 3
XLEAD = 2
RSLOTS = (0, 1)
HSLOT = 0
QSLOT = 0
GNORM = ("f",)
LATE = 3
T_MOST = 3
QUAD = 4
GROUPS = ((0, 3), (4, 5), (6, 6), (7, 7))
WORK_BUFS = 2

FLOPS = 3 * 2 * C * C * PIXELS


def flip(nc, psum, sbuf, identity, rows, which, copy):
    grouped = sbuf.tile([P, PACK, P, PACK], BF16, name="grouped_" + which, align_bytes=64)
    for j in range(PACK):
        flipped = psum.tile([P, PACK, P], BF16, name="flipped", tag="o", bufs=AHEAD_O)
        for t in range(PACK):
            nc.tensor.transpose(flipped[:, t, :], rows[:, j, t, :], identity[:])
        copy(out=grouped[:, j, :, :], in_=flipped[:].rearrange("q t p -> q p t"))
    return grouped


def flip_words(nc, psum, sbuf, identity_f32, rows, which, copy):
    words = rows[:].bitcast(F32).rearrange("p j (q u) -> p j u q", u=2)
    grouped = sbuf.tile([P, PACK, P, PACK], BF16, name="grouped_" + which, align_bytes=64)
    grouped_words = grouped[:].bitcast(F32)
    for j in range(PACK):
        flipped = psum.tile([P, 2, P], F32, name="flipped_words", tag="o", bufs=AHEAD_O)
        for u in range(2):
            nc.tensor.transpose(flipped[:, u, :], words[:, j, u, :], identity_f32[:])
        copy(out=grouped_words[:, j, :, :], in_=flipped[:].rearrange("q u p -> q p u"))
    return grouped


def quantise_matrix(nc, sbuf, grouped, which):
    codes = sbuf.tile([P, C], U32, name="codes_" + which, align_bytes=64)
    scales = sbuf.tile([P, C], U8, name="scales_" + which, align_bytes=64)
    nc.vector.quantize_mx(
        out=codes[:].bitcast(FP8X4),
        scales=scales[:],
        in_=grouped[:].rearrange("q j p t -> q (j p t)"),
    )
    return codes, scales


def row_maxima(nc, sbuf, score, which):
    negmax = sbuf.tile([P, PACK], F32, name="negmax_" + which)
    pairs = [slice(j, j + 2) for j in range(0, PACK, 2)]
    halves = []
    quarters = []
    for k, pair in enumerate(pairs):
        half = sbuf.tile([P, 2, C // 2], BF16, name="half_%d" % k)
        nc.vector.tensor_tensor(
            out=half[:], in0=score[:, pair, : C // 2], in1=score[:, pair, C // 2 :], op=ALU.max
        )
        halves.append(half)
    for k, half in enumerate(halves):
        quarter = sbuf.tile([P, 2, C // 4], BF16, name="quarter_%d" % k)
        nc.vector.tensor_tensor(
            out=quarter[:], in0=half[:, :, : C // 4], in1=half[:, :, C // 4 :], op=ALU.max
        )
        quarters.append(quarter)
    for pair, quarter in zip(pairs, quarters):
        nc.vector.tensor_reduce(
            out=negmax[:, pair], in_=quarter[:], axis=AXIS.X, op=ALU.max, negate=True
        )
    return negmax


def exponentials(nc, sbuf, early, score, negmax, which):
    e = early.tile([P, PACK, PACK, P], F32, name="e_" + which, tag="early")
    rowsum = sbuf.tile([P, PACK], F32, name="rowsum_" + which)
    for j in range(PACK):
        nc.scalar.activation(
            out=e[:, j, :, :].rearrange("p t q -> p q t"),
            in_=score[:, j, :].rearrange("p (q t) -> p q t", t=PACK),
            func=ACT.Exp,
            bias=negmax[:, j : j + 1],
            scale=1.0,
            accum_out=rowsum[:, j : j + 1],
        )
    return e, rowsum


def normalise(nc, sbuf, e, rowsum, which):
    inverse = sbuf.tile([P, PACK], F32, name="inverse_" + which)
    nc.vector.reciprocal(out=inverse[:], in_=rowsum[:])
    att = sbuf.tile([P, PACK, PACK, P], BF16, name="att_" + which)
    for j in range(PACK):
        if which in GNORM:
            nc.gpsimd.tensor_scalar(
                out=att[:, j, :, :], in0=e[:, j, :, :], scalar1=inverse[:, j : j + 1], scalar2=0.0,
                op0=ALU.mult, op1=ALU.add,
            )
        else:
            nc.scalar.activation(
                out=att[:, j, :, :], in_=e[:, j, :, :], func=ACT.Copy, scale=inverse[:, j : j + 1]
            )
    return att


def tile_coatten2_pb_t_kernel(tc, score_f, score_l, x_m, Wv, bv, gamma, x_f, x_l, out):
    nc = tc.nc
    with ExitStack() as stack:
        stack.enter_context(tc.manual_schedule())
        keep = stack.enter_context(tc.tile_pool(name="keep", bufs=1))
        early = stack.enter_context(tc.tile_pool(name="early", bufs=2))
        work = stack.enter_context(tc.tile_pool(name="work", bufs=WORK_BUFS))
        psum = stack.enter_context(tc.psum_pool(name="psum", bufs=2))

        identity_f32 = keep.tile([P, P], F32, name="identity_f32")
        make_identity(nc, identity_f32[:])
        identity = keep.tile([P, P], BF16, name="identity")
        make_identity(nc, identity[:])
        half_identity = keep.tile([P, P], BF16, name="half_identity")
        nc.vector.tensor_scalar_mul(out=half_identity[:], in0=identity[:], scalar1=0.5)

        def by_rows(matrix):
            return matrix.rearrange("(p j) n -> p j n", j=PACK)

        bias = keep.tile([P, PACK], BF16, name="bias")
        nc.scalar.dma_start(out=bias[:], in_=bv.rearrange("(p t) -> p t", t=PACK))
        gain_row = keep.tile([P, 2], BF16, name="gain_row")
        nc.gpsimd.memset(gain_row[:], 0.0)
        ones = keep.tile([P, P], BF16, name="ones")
        nc.gpsimd.memset(ones[:], 1.0)
        gain = keep.tile([P, 1], F32, name="gain")

        def load_matrix(matrix, which, parts):
            rows = keep.tile([P, PACK, C], BF16, name=which + "_rows")
            for j in range(0, PACK, PACK // parts):
                part = slice(j, j + PACK // parts)
                nc.sync.dma_start(out=rows[:, part, :], in_=by_rows(matrix)[:, part, :])
            return rows

        def load_chunk(matrix, which, k, chunks, pool=keep):
            piece = pool.tile([P, PACK, chunks * CHUNK], BF16, name="%s_%d" % (which, k), tag="%s_%d" % (which, k) if pool is keep else "early")
            nc.sync.dma_start(out=piece[:], in_=by_rows(matrix)[:, :, k * CHUNK : (k + chunks) * CHUNK])
            return [piece[:, :, c * CHUNK : (c + 1) * CHUNK] for c in range(chunks)]

        score_f_rows = load_matrix(score_f, "score_f", 2)
        xm = load_chunk(x_m, "xm", 0, 1)
        score_l_rows = load_matrix(score_l, "score_l", 1)
        wv_rows = load_matrix(Wv, "wv", 1)
        xm += load_chunk(x_m, "xm", 1, 1)
        nc.sync.dma_start(out=gain_row[0:1, 0:1], in_=gamma.unsqueeze(0))
        xm += load_chunk(x_m, "xm", 2, 2)
        xl = load_chunk(x_l, "xl", 0, 2)
        xf = load_chunk(x_f, "xf", 0, 2)
        for k in range(2, N_CHUNKS - 2, 2):
            xm += load_chunk(x_m, "xm", k + 2, 2)
            xl += load_chunk(x_l, "xl", k, 2)
            xf += load_chunk(x_f, "xf", k, 2)

        x_grouped = {}
        x_packed = {}
        v_grouped = {}
        v_packed = {}
        frame = {}
        quads = {}
        mean = {}
        product = {}
        attended = {}
        stationary = {}

        def quantise(grouped, which):
            codes = work.tile([P, CHUNK], U32, name=which + "_codes", align_bytes=64)
            scales = work.tile([P, CHUNK], U8, name=which + "_scales", align_bytes=64)
            nc.vector.quantize_mx(
                out=codes[:].bitcast(FP8X4),
                scales=scales[:],
                in_=grouped[:].rearrange("p n t -> p (n t)"),
            )
            return codes, scales

        def regroup_part(i, copy, h, parts):
            if h == 0:
                x_grouped[i] = work.tile([P, CHUNK, PACK], BF16, name="x_grouped", align_bytes=64)
            w = CHUNK // parts
            copy(
                out=x_grouped[i][:, h * w : (h + 1) * w, :].rearrange("p (c i) t -> p c t i", i=4),
                in_=xm[i][:, :, h * w : (h + 1) * w].rearrange("p t (c i) -> p c t i", i=4),
            )

        def project(u):
            i, s = divmod(u, PACK)
            codes, scales = x_packed[i]
            wv_codes, wv_scales = stationary["wv"]
            pixels = slice(s * SUB, (s + 1) * SUB)
            product[u] = psum.tile([P, PACK, SUB], F32, name="product", tag="v", bufs=AHEAD)
            for t in range(PACK):
                channels = slice(t * P, (t + 1) * P)
                nc.tensor.matmul_mx(
                    out=product[u][:, t, :],
                    lhsT=wv_codes[:, channels].bitcast(FP8X4),
                    lhsT_scale=wv_scales[:, channels],
                    rhs=codes[:, pixels].bitcast(FP8X4),
                    rhs_scale=scales[:, pixels],
                    start=True,
                    stop=True,
                )

        def add_bias(u):
            i, s = divmod(u, PACK)
            if s == 0:
                v_grouped[i] = work.tile([P, CHUNK, PACK], BF16, name="v_grouped", align_bytes=64)
            nc.vector.tensor_tensor(
                out=v_grouped[i][:, s * SUB : (s + 1) * SUB, :],
                in0=product[u][:].rearrange("p t n -> p n t"),
                in1=bias[:].unsqueeze(1).to_broadcast([P, SUB, PACK]),
                op=ALU.add,
            )

        def tensor_means(i):
            return 3 if i == 0 else 2

        def begin_frame(i):
            k = i // QUAD
            if k not in quads:
                quads[k] = keep.tile([P, PACK, QUAD * CHUNK], F32, name="frames_%d" % k)
            frame[i] = quads[k][:, :, (i % QUAD) * CHUNK : (i % QUAD + 1) * CHUNK]

        def mean_by_tensor(i, j):
            mean[i, j] = psum.tile([P, CHUNK], F32, name="mean", tag="m", bufs=2)
            nc.tensor.matmul(
                out=mean[i, j][:], lhsT=half_identity[:], rhs=xl[i][:, j, :], start=True, stop=False
            )
            nc.tensor.matmul(
                out=mean[i, j][:], lhsT=half_identity[:], rhs=xf[i][:, j, :], start=False, stop=True
            )

        def keep_mean(i, j):
            nc.scalar.copy(out=frame[i][:, j, :], in_=mean[i, j][:])

        def sum_by_gpsimd(i, j):
            nc.gpsimd.tensor_tensor(
                out=frame[i][:, j, :], in0=xl[i][:, j, :], in1=xf[i][:, j, :], op=ALU.add
            )

        def halve(i, j):
            nc.scalar.mul(out=frame[i][:, j, :], in_=frame[i][:, j, :], mul=0.5)

        def halve_by_gpsimd(i, j):
            nc.gpsimd.tensor_scalar(
                out=frame[i][:, j, :], in0=frame[i][:, j, :], scalar1=0.5, scalar2=0.0,
                op0=ALU.mult, op1=ALU.add,
            )

        def attend(u):
            i, j = divmod(u, PACK)
            codes, scales = v_packed[i]
            channels = slice(j * P, (j + 1) * P)
            attended[u] = psum.tile([P, CHUNK], F32, name="attended", tag="o", bufs=AHEAD_O)
            for which in ("f", "l"):
                att_codes, att_scales = stationary[which]
                nc.tensor.matmul_mx(
                    out=attended[u][:],
                    lhsT=att_codes[:, channels].bitcast(FP8X4),
                    lhsT_scale=att_scales[:, channels],
                    rhs=codes[:].bitcast(FP8X4),
                    rhs_scale=scales[:],
                    start=(which == "f"),
                    stop=(which == "l"),
                )

        def by_scalar(u):
            i, j = divmod(u, PACK)
            return j == 1 and i <= 4

        scaled = {}

        def fuse_s(u):
            if by_scalar(u):
                scaled[u] = work.tile([P, CHUNK], F32, name="scaled")
                nc.scalar.activation(out=scaled[u][:], in_=attended[u][:], func=ACT.Copy, scale=gain[:, 0:1])

        def fuse(u):
            i, j = divmod(u, PACK)
            if by_scalar(u):
                nc.gpsimd.tensor_tensor(
                    out=frame[i][:, j, :], in0=scaled[u][:], in1=frame[i][:, j, :], op=ALU.add
                )
            else:
                nc.vector.scalar_tensor_tensor(
                    out=frame[i][:, j, :],
                    in0=attended[u][:],
                    scalar=gain[:, 0:1],
                    in1=frame[i][:, j, :],
                    op0=ALU.mult,
                    op1=ALU.add,
                )
            if by_scalar(u):
                late.append(u)
            else:
                store(u)

        late = []

        def store(u):
            i, j = divmod(u, PACK)
            for first, last in GROUPS:
                if i == last:
                    k = first % QUAD
                    nc.sync.dma_start(
                        out=by_rows(out)[:, j, first * CHUNK : (last + 1) * CHUNK],
                        in_=quads[i // QUAD][:, j, k * CHUNK : (k + last - first + 1) * CHUNK],
                    )

        def store_late(u):
            for v in [v for v in late if v <= u]:
                store(v)
                late.remove(v)

        def is_chunk(i):
            return 0 <= i < N_CHUNKS

        def is_bank(u):
            return 0 <= u < N_BANKS

        def bias_bank(u):
            add_bias(u)
            if is_bank(u + AHEAD):
                project(u + AHEAD)

        waiting = []
        summed = []
        tensor_jobs = [(i, j) for i in range(1, N_CHUNKS) for j in range(tensor_means(i))]
        gpsimd_jobs = [(i, j) for i in range(1, N_CHUNKS) for j in range(tensor_means(i), PACK)]

        def take(jobs, most, last_chunk):
            taken = [job for job in jobs[:most] if job[0] <= last_chunk]
            for job in taken:
                jobs.remove(job)
                begin_frame(job[0])
            return taken

        def cycle(n):
            means = take(tensor_jobs, T_MOST, n if n >= N_CHUNKS - 2 else n - 1)
            sums = take(gpsimd_jobs, 2, n if n > 2 else n - 1)
            halves = list(summed)
            summed.clear()
            summed.extend(sums)
            for s in range(PACK):
                u = n * PACK + s
                if is_bank(u - LAG):
                    fuse_s(u - LAG)
                for job in waiting:
                    keep_mean(*job)
                waiting.clear()
                if s in RSLOTS and is_chunk(n + XLEAD):
                    regroup_part(n + XLEAD, nc.scalar.copy, RSLOTS.index(s), len(RSLOTS))
                if is_bank(u):
                    bias_bank(u)
                if is_bank(u - LAG):
                    fuse(u - LAG)
                    store_late(u - LAG - LATE)
                for job in means[s::PACK]:
                    mean_by_tensor(*job)
                    waiting.append(job)
                if s == QSLOT:
                    if is_chunk(n - 1):
                        v_packed[n - 1] = quantise(v_grouped[n - 1], "v")
                    if is_chunk(n + 1):
                        x_packed[n + 1] = quantise(x_grouped[n + 1], "x")
                    if sums:
                        i, j = sums[0]
                        nc.vector.memset(frame[i][:, j, 0:1], 0.0)
                    for job in sums:
                        sum_by_gpsimd(*job)
                if is_bank(u - LAG + AHEAD_O):
                    attend(u - LAG + AHEAD_O)
                if s == HSLOT:
                    for job in halves:
                        halve(*job)

        def regroup(i, copy):
            regroup_part(i, copy, 0, 1)

        def pack_x(i):
            x_packed[i] = quantise(x_grouped[i], "x")

        negmax_f = row_maxima(nc, keep, score_f_rows, "f")
        e_f, sum_f = exponentials(nc, keep, early, score_f_rows, negmax_f, "f")
        regroup(0, nc.vector.tensor_copy)
        pack_x(0)
        wv_grouped = flip_words(nc, psum, keep, identity_f32, wv_rows, "wv", nc.scalar.copy)
        negmax_l = row_maxima(nc, keep, score_l_rows, "l")
        e_l, sum_l = exponentials(nc, keep, early, score_l_rows, negmax_l, "l")
        regroup(1, nc.vector.tensor_copy)
        stationary["wv"] = quantise_matrix(nc, keep, wv_grouped, "wv")
        for u in range(AHEAD):
            project(u)
        pack_x(1)
        att_f = normalise(nc, keep, e_f, sum_f, "f")
        begin_frame(0)
        for j in range(tensor_means(0), PACK):
            sum_by_gpsimd(0, j)
            halve_by_gpsimd(0, j)
        bias_bank(0)
        att_l = normalise(nc, keep, e_l, sum_l, "l")
        regroup_part(2, nc.scalar.copy, 0, 2)
        for u in range(1, 2 * PACK - AHEAD):
            bias_bank(u)
        spread = psum.tile([P, 2], F32, name="spread", tag="m", bufs=2)
        nc.tensor.matmul(out=spread[:], lhsT=ones[:], rhs=gain_row[:], start=True, stop=True)
        nc.scalar.copy(out=gain[:], in_=spread[:, 0:1])
        f_grouped = flip(nc, psum, keep, identity, att_f, "f", nc.scalar.copy)
        for u in range(2 * PACK - AHEAD, 2 * PACK):
            add_bias(u)
        v_packed[0] = quantise(v_grouped[0], "v")
        regroup_part(2, nc.vector.tensor_copy, 1, 2)
        pack_x(2)
        l_grouped = flip(nc, psum, keep, identity, att_l, "l", nc.scalar.copy)
        mean_by_tensor(0, 0)
        mean_by_tensor(0, 1)
        keep_mean(0, 0)
        keep_mean(0, 1)
        for u in range(2 * PACK, 2 * PACK + AHEAD):
            project(u)
        stationary["f"] = quantise_matrix(nc, keep, f_grouped, "f")
        stationary["l"] = quantise_matrix(nc, keep, l_grouped, "l")
        for u in range(AHEAD_O):
            attend(u)
        regroup(3, nc.scalar.copy)
        for j in range(2, tensor_means(0)):
            mean_by_tensor(0, j)
            keep_mean(0, j)
        xl += load_chunk(x_l, "xl", N_CHUNKS - 2, 2, early)
        xf += load_chunk(x_f, "xf", N_CHUNKS - 2, 2, early)
        for n in range(2, N_CHUNKS + LAG // PACK):
            cycle(n)
        store_late(N_BANKS)
